import numpy as np
import ml_dtypes


def mxq(x, axis, fmt="e4m3"):
    dtype, down = {"e4m3": (ml_dtypes.float8_e4m3fn, 7), "e5m2": (ml_dtypes.float8_e5m2, 14)}[fmt]
    v = np.moveaxis(np.asarray(x, np.float32).astype(ml_dtypes.bfloat16).astype(np.float64), axis, -1)
    blocks = v.reshape(v.shape[:-1] + (-1, 32))
    amax = np.abs(blocks).max(-1, keepdims=True)
    byte = np.maximum(np.where(amax > 0, np.frexp(amax)[1] - 1 + 127, 0) - down, 1)
    scale = np.exp2(byte - 127.0)
    codes = (blocks / scale).astype(np.float32).astype(dtype).astype(np.float64)
    return np.moveaxis((codes * scale).reshape(v.shape), -1, axis)


WIDE = False


def mx_kscale(k):
    if not WIDE:
        return np.ones(k)
    levels = np.array([10, -10, 5, -5, 0])
    a = np.random.permutation(np.resize(levels, k // 512 * 4)).reshape(k // 512, 4)
    idx = np.arange(k)
    return np.exp2(a[idx // 512, idx % 128 // 32])


BF16 = ml_dtypes.bfloat16


def bf(x):
    return np.asarray(x, np.float32).astype(BF16)


def f64(x):
    return np.asarray(x).astype(np.float64)


B, C, O, H, W, KH, KW, PAD = 4, 512, 512, 16, 16, 3, 3, 1
C_CURV = 0.01
EPS = 1e-7


def artanh(z):
    return 0.5 * np.log((1.0 + z) / (1.0 - z))


def log0(y):
    sqc = np.sqrt(C_CURV)
    n = np.maximum(np.sqrt((y * y).sum(-1, keepdims=True)), EPS)
    return artanh(np.clip(sqc * n, 0.0, 1.0 - 1e-6)) * y / (sqc * n)


def exp0(v):
    sqc = np.sqrt(C_CURV)
    n = np.maximum(np.sqrt((v * v).sum(-1, keepdims=True)), EPS)
    return np.tanh(sqc * n) * v / (sqc * n)


def setup_inputs():
    s = mx_kscale(C)
    rho = np.sqrt(np.mean(s * s))
    raw = np.random.uniform(0.0, 1.0, (B, C, H, W)) * s[None, :, None, None]
    r = np.random.uniform(0.2, 0.85, (B, 1, H, W))
    x = raw / np.sqrt((raw * raw).sum(1, keepdims=True)) * r / np.sqrt(C_CURV)
    return {"x": bf(x),
            "Wk": bf(np.random.standard_normal((KH * KW, O, C)) * 2.1 / np.sqrt(KH * KW * O) * rho / s),
            "bias": bf(np.random.standard_normal(O) * 5.0 / np.sqrt(O))}


def reference(x, Wk, bias):
    Hout, Wout = H + 2 * PAD - KH + 1, W + 2 * PAD - KW + 1
    u = log0(np.moveaxis(f64(x), 1, -1)).reshape(B * H * W, C)
    w = f64(Wk).transpose(2, 0, 1).reshape(C, KH * KW * O)
    y = mxq(u, 1, "e4m3") @ mxq(w, 0, "e4m3")
    yp = np.pad(y.reshape(B, H, W, KH * KW, O), ((0, 0), (PAD, PAD), (PAD, PAD), (0, 0), (0, 0)))
    v = sum(yp[:, i:i + Hout, j:j + Wout, KW * i + j, :] for i in range(KH) for j in range(KW))
    v = np.maximum(v + f64(bias), 0.0)
    out = exp0(v)
    return np.transpose(out, (0, 3, 1, 2))

@@ -1,0 +1,255 @@
+from contextlib import ExitStack
+
+import concourse.bass as bass
+import concourse.mybir as mybir
+import concourse.tile as tile
+from concourse.masks import make_identity
+
+F32 = mybir.dt.float32
+BF16 = mybir.dt.bfloat16
+U32 = mybir.dt.uint32
+U8 = mybir.dt.uint8
+I32 = mybir.dt.int32
+FP8X4 = mybir.dt.float8_e4m3fn_x4
+ALU = mybir.AluOpType
+ACT = mybir.ActivationFunctionType
+AX = mybir.AxisListType
+
+P = 128
+B, C, O, H, W = 4, 512, 512, 16, 16
+HW = H * W
+ROW = B * W
+NPOS = 9
+FLOPS = 2 * B * HW * C * NPOS * O
+
+
+def tile_pvconv2d_kernel(tc, x, Wk, bias, out):
+    nc = tc.nc
+    with ExitStack() as ctx:
+        const = ctx.enter_context(tc.tile_pool(name="const", bufs=1))
+        big = ctx.enter_context(tc.tile_pool(name="big", bufs=1))
+        stage = ctx.enter_context(tc.tile_pool(name="stage", bufs=3))
+        small = ctx.enter_context(tc.tile_pool(name="small", bufs=1))
+        tsmall = ctx.enter_context(tc.tile_pool(name="tsmall", bufs=4))
+        psum = ctx.enter_context(tc.psum_pool(name="psum", bufs=8))
+
+        x_sb = big.tile([P, B, 4, HW], BF16)
+        for b in range(B):
+            nc.sync.dma_start(
+                out=x_sb[:, b].rearrange("p (u e) q -> p u (e q)", u=2),
+                in_=x[b].rearrange("(u p e) h w -> p u (e h w)", u=2, e=2),
+            )
+        w_sb = []
+        for k in range(NPOS):
+            wk = big.tile([P, 4 * C], BF16, name="w_sb%d" % k)
+            nc.sync.dma_start(out=wk[:], in_=Wk[k].rearrange("(n ot) c -> n (ot c)", ot=4))
+            w_sb.append(wk)
+
+        ident = const.tile([P, P], F32)
+        make_identity(nc, ident[:])
+        perm = const.tile([P, P], F32)
+        nc.gpsimd.tensor_copy(
+            out=perm[:].rearrange("p (b hh w) -> p b hh w", b=B, hh=2),
+            in_=ident[:].rearrange("p (hh b w) -> p b hh w", hh=2, b=B),
+        )
+        half = const.tile([P, 8], F32)
+        nc.gpsimd.memset(half[:], 0.5)
+        ones_bf = const.tile([P, P], BF16)
+        nc.gpsimd.memset(ones_bf[:], 1.0)
+        bias_row = const.tile([P, O], BF16)
+        nc.gpsimd.memset(bias_row[:], 0.0)
+        nc.scalar.dma_start(out=bias_row[0:1, :], in_=bias.unsqueeze(0))
+        junk = const.tile([P, 8], F32)
+        nc.scalar.activation(out=junk[:], in_=half[:], func=ACT.Ln)
+
+        g_t = []
+        uq = []
+        us = []
+        for j in range(3):
+            g_t.append(big.tile([P, H, B, W, 4], BF16, name="g%d" % j, align_bytes=64))
+            uq.append(big.tile([P, (H + 2) * ROW], U32, name="uq%d" % j, align_bytes=64))
+            us.append(big.tile([P, (H + 2) * ROW], U8, name="us%d" % j, align_bytes=64))
+        for j in range(3):
+            nc.vector.memset(us[j][:].bitcast(I32), 0)
+            nc.vector.memset(uq[j][:, 0:ROW].bitcast(I32), 0)
+            nc.vector.memset(uq[j][:, (H + 1) * ROW:(H + 2) * ROW].bitcast(I32), 0)
+        nc.vector.memset(g_t[0][:], 0.0)
+        nc.vector.memset(g_t[2][:], 0.0)
+
+        n2 = small.tile([P, 8], F32)
+        for g in range(2):
+            gram = psum.tile([P, 4, P], F32, tag="ps")
+            for mm in range(4):
+                m = 4 * g + mm
+                b, hf = divmod(m, 2)
+                for t in range(4):
+                    blk = x_sb[:, b, t, hf * P:(hf + 1) * P]
+                    nc.tensor.matmul(out=gram[:, mm, :], lhsT=blk, rhs=blk, start=(t == 0), stop=(t == 3))
+            dg = stage.tile([P, 4, P], F32, tag="dg")
+            nc.vector.tensor_tensor(
+                out=dg[:], in0=gram[:], in1=ident[:].unsqueeze(1).to_broadcast([P, 4, P]), op=ALU.mult
+            )
+            nc.vector.tensor_reduce(out=n2[:, 4 * g:4 * g + 4], in_=dg[:], axis=AX.X, op=ALU.add)
+
+        n2c = small.tile([P, 8], F32)
+        nc.vector.tensor_scalar(out=n2c[:], in0=n2[:], scalar1=1e-14, scalar2=None, op0=ALU.max)
+        nrm = small.tile([P, 8], F32)
+        nc.gpsimd.tensor_tensor(out=nrm[:], in0=n2c[:], in1=half[:], op=ALU.pow)
+        z = small.tile([P, 8], F32)
+        nc.vector.tensor_scalar(out=z[:], in0=nrm[:], scalar1=0.1, scalar2=1.0 - 1e-6, op0=ALU.mult, op1=ALU.min)
+        l1 = small.tile([P, 8], F32)
+        nc.scalar.activation(out=l1[:], in_=z[:], func=ACT.Ln, bias=1.0, scale=1.0)
+        l2 = small.tile([P, 8], F32)
+        nc.scalar.activation(out=l2[:], in_=z[:], func=ACT.Ln, bias=1.0, scale=-1.0)
+        junk2 = const.tile([P, 8], F32)
+        nc.scalar.activation(out=junk2[:], in_=l2[:], func=ACT.Tanh)
+        rec = small.tile([P, 8], F32)
+        nc.vector.reciprocal(out=rec[:], in_=nrm[:])
+        dl = small.tile([P, 8], F32)
+        nc.vector.tensor_tensor(out=dl[:], in0=l1[:], in1=l2[:], op=ALU.subtract)
+        s = small.tile([P, 8], F32)
+        nc.vector.scalar_tensor_tensor(out=s[:], in0=dl[:], scalar=5.0, in1=rec[:], op0=ALU.mult, op1=ALU.mult)
+
+        sbc = []
+        for g in range(2):
+            sb_t = psum.tile([P, 4 * P], F32, tag="ps")
+            for mm in range(4):
+                m = 4 * g + mm
+                nc.tensor.transpose(sb_t[:, mm * P:(mm + 1) * P], s[:, m:m + 1].to_broadcast([P, P]), ident[:])
+            sbc.append(sb_t)
+
+        flat = [g_t[j][:].rearrange("p h b w t -> p (h b) (w t)") for j in range(3)]
+        line = [g_t[j][:].rearrange("p h b w t -> p (h b w t)") for j in range(3)]
+
+        def make_u(h0, nh):
+            for b in range(B):
+                nc.vector.tensor_tensor(
+                    out=g_t[1][:, h0:h0 + nh, b, :, :],
+                    in0=x_sb[:, b, :, h0 * W:(h0 + nh) * W].rearrange("p t (h w) -> p h w t", h=nh),
+                    in1=sbc[b // 2][:, (b % 2) * HW + h0 * W:(b % 2) * HW + (h0 + nh) * W]
+                    .rearrange("p (h w) -> p h w", h=nh)
+                    .unsqueeze(3)
+                    .to_broadcast([P, nh, W, 4]),
+                    op=ALU.mult,
+                )
+            r0, r1 = h0 * B, (h0 + nh) * B
+            nc.scalar.copy(out=flat[0][:, r0:r1, 4:64], in_=flat[1][:, r0:r1, 0:60])
+            nc.scalar.copy(out=flat[2][:, r0:r1, 0:60], in_=flat[1][:, r0:r1, 4:64])
+            for j in (1, 0, 2):
+                nc.vector.quantize_mx(
+                    out=uq[j][:, (h0 + 1) * ROW:(h0 + nh + 1) * ROW].bitcast(FP8X4),
+                    scales=us[j][:, (h0 + 1) * ROW:(h0 + nh + 1) * ROW],
+                    in_=line[j][:, h0 * ROW * 4:(h0 + nh) * ROW * 4],
+                )
+
+        make_u(0, 4)
+        make_u(4, 4)
+
+        wq = []
+        ws = []
+        for k in range(NPOS):
+            wf = w_sb[k][:].bitcast(F32)
+            wg = stage.tile([P, 4 * O], BF16, tag="wg", align_bytes=64)
+            wgf = wg[:].bitcast(F32)
+            for hh in range(2):
+                wt = psum.tile([P, 2, 2 * P], F32, tag="ps")
+                for u in range(2):
+                    for o2 in range(2):
+                        ot = 2 * hh + o2
+                        nc.tensor.transpose(
+                            wt[:, u, o2 * P:(o2 + 1) * P],
+                            wf[:, 256 * ot + P * u:256 * ot + P * u + P],
+                            ident[:],
+                        )
+                if k < 3 and hh == 1:
+                    nc.vector.tensor_copy(
+                        out=wgf[:, hh * 512:(hh + 1) * 512].rearrange("p (c u) -> p c u", u=2),
+                        in_=wt[:].rearrange("p u c -> p c u"),
+                    )
+                else:
+                    nc.scalar.copy(
+                        out=wgf[:, hh * 512:(hh + 1) * 512].rearrange("p (c u) -> p c u", u=2),
+                        in_=wt[:].rearrange("p u c -> p c u"),
+                    )
+            wqk = big.tile([P, O], U32, name="wq%d" % k, align_bytes=64)
+            wsk = big.tile([P, O], U8, name="ws%d" % k, align_bytes=64)
+            nc.vector.quantize_mx(out=wqk[:].bitcast(FP8X4), scales=wsk[:], in_=wg[:])
+            wq.append(wqk)
+            ws.append(wsk)
+
+        make_u(8, 8)
+
+        pb = psum.tile([P, O], F32, tag="ps")
+        nc.tensor.matmul(out=pb[:], lhsT=ones_bf[:], rhs=bias_row[:], start=True, stop=True)
+        bias_bc = const.tile([P, O], F32)
+        nc.vector.tensor_copy(
+            out=bias_bc[:].rearrange("p (ot n) -> p ot n", ot=4),
+            in_=pb[:].rearrange("p (n ot) -> p ot n", ot=4),
+        )
+
+        o_sb = big.tile([P, B, 4, HW], F32)
+        out_v = out.rearrange("b (n ot) h w -> b n ot (h w)", ot=4)
+
+        def mx_pass(acc, T, k):
+            i, j = divmod(k, 3)
+            c0 = (2 * T + i) * ROW
+            nc.tensor.matmul_mx(
+                out=acc[:],
+                lhsT=uq[j][:, c0:c0 + P].bitcast(FP8X4),
+                lhsT_scale=us[j][:, c0:c0 + P],
+                rhs=wq[k][:].bitcast(FP8X4),
+                rhs_scale=ws[k][:],
+                start=(k == 0),
+                stop=(k == NPOS - 1),
+            )
+
+        def tail(acc, T):
+            t_sb = stage.tile([P, O], F32, tag="t")
+            nc.vector.tensor_tensor(out=t_sb[:], in0=acc[:], in1=bias_bc[:], op=ALU.add)
+            sq = stage.tile([P, O], F32, tag="sq")
+            m2 = tsmall.tile([P, 1], F32, tag="m2")
+            nc.vector.scalar_tensor_tensor(
+                out=sq[:], in0=t_sb[:], scalar=0.0, in1=t_sb[:], op0=ALU.max, op1=ALU.mult, accum_out=m2[:]
+            )
+            m2c = tsmall.tile([P, 1], F32, tag="m2c")
+            nc.vector.tensor_scalar(out=m2c[:], in0=m2[:], scalar1=1e-14, scalar2=None, op0=ALU.max)
+            mn = tsmall.tile([P, 1], F32, tag="mn")
+            nc.gpsimd.tensor_tensor(out=mn[:], in0=m2c[:], in1=half[:, 0:1], op=ALU.pow)
+            th = tsmall.tile([P, 1], F32, tag="th")
+            nc.scalar.activation(out=th[:], in_=mn[:], func=ACT.Tanh, scale=0.1)
+            mr = tsmall.tile([P, 1], F32, tag="mr")
+            nc.vector.reciprocal(out=mr[:], in_=mn[:])
+            gs = tsmall.tile([P, 1], F32, tag="gs")
+            nc.vector.scalar_tensor_tensor(
+                out=gs[:], in0=th[:], scalar=10.0, in1=mr[:], op0=ALU.mult, op1=ALU.mult
+            )
+            rs = stage.tile([P, O], F32, tag="rs")
+            nc.scalar.activation(out=rs[:], in_=t_sb[:], func=ACT.Relu, scale=gs[:, 0:1])
+            pt = psum.tile([P, O], F32, tag="ps")
+            for ot in range(4):
+                nc.tensor.transpose(pt[:, ot * P:(ot + 1) * P], rs[:, ot * P:(ot + 1) * P], perm[:])
+            nc.scalar.copy(
+                out=o_sb[:, :, :, 32 * T:32 * T + 32],
+                in_=pt[:].rearrange("p (ot b q) -> p b ot q", ot=4, b=B),
+            )
+
+        def store(q0, q1):
+            for b in range(B):
+                nc.sync.dma_start(out=out_v[b][:, :, q0:q1], in_=o_sb[:, b, :, q0:q1])
+
+        first = [psum.tile([P, O], F32, tag="ps", name="acc%d" % T) for T in range(3)]
+        for k in range(NPOS):
+            for T in range(3):
+                mx_pass(first[T], T, k)
+        for T in range(3):
+            tail(first[T], T)
+        store(0, 64)
+        for T in range(3, 8):
+            acc = psum.tile([P, O], F32, tag="ps")
+            for k in range(NPOS):
+                mx_pass(acc, T, k)
+            tail(acc, T)
+            if T in (3, 5):
+                store(32 * (T - 1), 32 * (T + 1))
+            if T in (6, 7):
+                store(32 * T, 32 * (T + 1))

@@ -31,44 +31,49 @@ def tile_pvconv2d_kernel(tc, x, Wk, bias, out):
         stage = ctx.enter_context(tc.tile_pool(name="stage", bufs=3))
         small = ctx.enter_context(tc.tile_pool(name="small", bufs=1))
         tsmall = ctx.enter_context(tc.tile_pool(name="tsmall", bufs=4))
-        psum = ctx.enter_context(tc.psum_pool(name="psum", bufs=8))
+        ps_hd = ctx.enter_context(tc.psum_pool(name="ps_hd", bufs=2))
+        ps_wt = ctx.enter_context(tc.psum_pool(name="ps_wt", bufs=3))
+        ps_acc = ctx.enter_context(tc.psum_pool(name="ps_acc", bufs=3))
+        ctx.enter_context(tc.manual_schedule())
 
         x_sb = big.tile([P, B, 4, HW], BF16)
+        w_sb = [big.tile([P, 4 * C], BF16, name="w_sb%d" % k) for k in range(NPOS)]
+        wq = [big.tile([P, O], U32, name="wq%d" % k, align_bytes=64) for k in range(NPOS)]
+        ws = [big.tile([P, O], U8, name="ws%d" % k, align_bytes=64) for k in range(NPOS)]
+        g_t = [big.tile([P, H, B, W, 4], BF16, name="g%d" % j, align_bytes=64) for j in range(3)]
+        uq = [big.tile([P, (H + 2) * ROW], U32, name="uq%d" % j, align_bytes=64) for j in range(3)]
+        us = [big.tile([P, (H + 2) * ROW], U8, name="us%d" % j, align_bytes=64) for j in range(3)]
+        o_sb = big.tile([P, B, 4, HW], F32)
+        out_v = out.rearrange("b (n ot) h w -> b n ot (h w)", ot=4)
+        ident = const.tile([P, P], F32)
+        perm = const.tile([P, P], F32)
+        half = const.tile([P, 8], F32)
+        mhalf = const.tile([P, 8], F32)
+        ones_bf = const.tile([P, P], BF16)
+        bias_row = const.tile([P, O], BF16)
+        bias_bc = const.tile([P, O], F32)
+        junk = const.tile([P, 8], F32)
+        flat = [g_t[j][:].rearrange("p h b w t -> p (h b) (w t)") for j in range(3)]
+        line = [g_t[j][:].rearrange("p h b w t -> p (h b w t)") for j in range(3)]
+
         for b in range(B):
             nc.sync.dma_start(
                 out=x_sb[:, b].rearrange("p (u e) q -> p u (e q)", u=2),
                 in_=x[b].rearrange("(u p e) h w -> p u (e h w)", u=2, e=2),
             )
-        w_sb = []
         for k in range(NPOS):
-            wk = big.tile([P, 4 * C], BF16, name="w_sb%d" % k)
-            nc.sync.dma_start(out=wk[:], in_=Wk[k].rearrange("(n ot) c -> n (ot c)", ot=4))
-            w_sb.append(wk)
-
-        ident = const.tile([P, P], F32)
+            nc.sync.dma_start(out=w_sb[k][:], in_=Wk[k].rearrange("(n ot) c -> n (ot c)", ot=4))
         make_identity(nc, ident[:])
-        perm = const.tile([P, P], F32)
+        nc.gpsimd.memset(half[:], 0.5)
+        nc.gpsimd.memset(mhalf[:], -0.5)
+        nc.gpsimd.memset(bias_row[:], 0.0)
+        nc.scalar.dma_start(out=bias_row[0:1, :], in_=bias.unsqueeze(0))
+        nc.gpsimd.memset(ones_bf[:], 1.0)
         nc.gpsimd.tensor_copy(
             out=perm[:].rearrange("p (b hh w) -> p b hh w", b=B, hh=2),
             in_=ident[:].rearrange("p (hh b w) -> p b hh w", hh=2, b=B),
         )
-        half = const.tile([P, 8], F32)
-        nc.gpsimd.memset(half[:], 0.5)
-        ones_bf = const.tile([P, P], BF16)
-        nc.gpsimd.memset(ones_bf[:], 1.0)
-        bias_row = const.tile([P, O], BF16)
-        nc.gpsimd.memset(bias_row[:], 0.0)
-        nc.scalar.dma_start(out=bias_row[0:1, :], in_=bias.unsqueeze(0))
-        junk = const.tile([P, 8], F32)
         nc.scalar.activation(out=junk[:], in_=half[:], func=ACT.Ln)
-
-        g_t = []
-        uq = []
-        us = []
-        for j in range(3):
-            g_t.append(big.tile([P, H, B, W, 4], BF16, name="g%d" % j, align_bytes=64))
-            uq.append(big.tile([P, (H + 2) * ROW], U32, name="uq%d" % j, align_bytes=64))
-            us.append(big.tile([P, (H + 2) * ROW], U8, name="us%d" % j, align_bytes=64))
         for j in range(3):
             nc.vector.memset(us[j][:].bitcast(I32), 0)
             nc.vector.memset(uq[j][:, 0:ROW].bitcast(I32), 0)
@@ -76,53 +81,62 @@ def tile_pvconv2d_kernel(tc, x, Wk, bias, out):
         nc.vector.memset(g_t[0][:], 0.0)
         nc.vector.memset(g_t[2][:], 0.0)
 
-        n2 = small.tile([P, 8], F32)
-        for g in range(2):
-            gram = psum.tile([P, 4, P], F32, tag="ps")
+        n2 = [small.tile([P, 4], F32, name="n2_%d" % g) for g in range(2)]
+        n2c = [small.tile([P, 4], F32, name="n2c_%d" % g) for g in range(2)]
+        nrm = [small.tile([P, 4], F32, name="nrm_%d" % g) for g in range(2)]
+        z = [small.tile([P, 4], F32, name="z_%d" % g) for g in range(2)]
+        l1 = [small.tile([P, 4], F32, name="l1_%d" % g) for g in range(2)]
+        l2 = [small.tile([P, 4], F32, name="l2_%d" % g) for g in range(2)]
+        rec = [small.tile([P, 4], F32, name="rec_%d" % g) for g in range(2)]
+        dl = [small.tile([P, 4], F32, name="dl_%d" % g) for g in range(2)]
+        s = [small.tile([P, 4], F32, name="s_%d" % g) for g in range(2)]
+        grams = {}
+        sbc = {}
+
+        def gram_pe(g):
+            grams[g] = ps_hd.tile([P, 4, P], F32, tag="hd", name="gram")
             for mm in range(4):
-                m = 4 * g + mm
-                b, hf = divmod(m, 2)
+                b, hf = divmod(4 * g + mm, 2)
                 for t in range(4):
                     blk = x_sb[:, b, t, hf * P:(hf + 1) * P]
-                    nc.tensor.matmul(out=gram[:, mm, :], lhsT=blk, rhs=blk, start=(t == 0), stop=(t == 3))
+                    nc.tensor.matmul(out=grams[g][:, mm, :], lhsT=blk, rhs=blk, start=(t == 0), stop=(t == 3))
+
+        def gram_diag(g):
             dg = stage.tile([P, 4, P], F32, tag="dg")
             nc.vector.tensor_tensor(
-                out=dg[:], in0=gram[:], in1=ident[:].unsqueeze(1).to_broadcast([P, 4, P]), op=ALU.mult
+                out=dg[:], in0=grams[g][:], in1=ident[:].unsqueeze(1).to_broadcast([P, 4, P]), op=ALU.mult
             )
-            nc.vector.tensor_reduce(out=n2[:, 4 * g:4 * g + 4], in_=dg[:], axis=AX.X, op=ALU.add)
+            nc.vector.tensor_reduce(out=n2[g][:], in_=dg[:], axis=AX.X, op=ALU.add)
+            nc.vector.tensor_scalar(out=n2c[g][:], in0=n2[g][:], scalar1=1e-14, scalar2=None, op0=ALU.max)
 
-        n2c = small.tile([P, 8], F32)
-        nc.vector.tensor_scalar(out=n2c[:], in0=n2[:], scalar1=1e-14, scalar2=None, op0=ALU.max)
-        nrm = small.tile([P, 8], F32)
-        nc.gpsimd.tensor_tensor(out=nrm[:], in0=n2c[:], in1=half[:], op=ALU.pow)
-        z = small.tile([P, 8], F32)
-        nc.vector.tensor_scalar(out=z[:], in0=nrm[:], scalar1=0.1, scalar2=1.0 - 1e-6, op0=ALU.mult, op1=ALU.min)
-        l1 = small.tile([P, 8], F32)
-        nc.scalar.activation(out=l1[:], in_=z[:], func=ACT.Ln, bias=1.0, scale=1.0)
-        l2 = small.tile([P, 8], F32)
-        nc.scalar.activation(out=l2[:], in_=z[:], func=ACT.Ln, bias=1.0, scale=-1.0)
-        junk2 = const.tile([P, 8], F32)
-        nc.scalar.activation(out=junk2[:], in_=l2[:], func=ACT.Tanh)
-        rec = small.tile([P, 8], F32)
-        nc.vector.reciprocal(out=rec[:], in_=nrm[:])
-        dl = small.tile([P, 8], F32)
-        nc.vector.tensor_tensor(out=dl[:], in0=l1[:], in1=l2[:], op=ALU.subtract)
-        s = small.tile([P, 8], F32)
-        nc.vector.scalar_tensor_tensor(out=s[:], in0=dl[:], scalar=5.0, in1=rec[:], op0=ALU.mult, op1=ALU.mult)
+        def c_pow(g):
+            nc.gpsimd.tensor_tensor(out=nrm[g][:], in0=n2c[g][:], in1=half[:, 0:4], op=ALU.pow)
 
-        sbc = []
-        for g in range(2):
-            sb_t = psum.tile([P, 4 * P], F32, tag="ps")
+        def c_z(g):
+            nc.vector.tensor_scalar(
+                out=z[g][:], in0=nrm[g][:], scalar1=0.1, scalar2=1.0 - 1e-6, op0=ALU.mult, op1=ALU.min
+            )
+            nc.vector.reciprocal(out=rec[g][:], in_=nrm[g][:])
+
+        def c_ln(g):
+            nc.scalar.activation(out=l1[g][:], in_=z[g][:], func=ACT.Ln, bias=1.0, scale=1.0)
+            nc.scalar.activation(out=l2[g][:], in_=z[g][:], func=ACT.Ln, bias=1.0, scale=-1.0)
+
+        def c_s(g):
+            nc.vector.tensor_tensor(out=dl[g][:], in0=l1[g][:], in1=l2[g][:], op=ALU.subtract)
+            nc.vector.scalar_tensor_tensor(
+                out=s[g][:], in0=dl[g][:], scalar=5.0, in1=rec[g][:], op0=ALU.mult, op1=ALU.mult
+            )
+
+        def spread(g):
+            sbc[g] = ps_hd.tile([P, 4 * P], F32, tag="hd", name="sbc")
             for mm in range(4):
-                m = 4 * g + mm
-                nc.tensor.transpose(sb_t[:, mm * P:(mm + 1) * P], s[:, m:m + 1].to_broadcast([P, P]), ident[:])
-            sbc.append(sb_t)
+                nc.tensor.transpose(
+                    sbc[g][:, mm * P:(mm + 1) * P], s[g][:, mm:mm + 1].to_broadcast([P, P]), ident[:]
+                )
 
-        flat = [g_t[j][:].rearrange("p h b w t -> p (h b) (w t)") for j in range(3)]
-        line = [g_t[j][:].rearrange("p h b w t -> p (h b w t)") for j in range(3)]
-
-        def make_u(h0, nh):
-            for b in range(B):
+        def u_mul(h0, nh, bs):
+            for b in bs:
                 nc.vector.tensor_tensor(
                     out=g_t[1][:, h0:h0 + nh, b, :, :],
                     in0=x_sb[:, b, :, h0 * W:(h0 + nh) * W].rearrange("p t (h w) -> p h w t", h=nh),
@@ -132,27 +146,38 @@ def tile_pvconv2d_kernel(tc, x, Wk, bias, out):
                     .to_broadcast([P, nh, W, 4]),
                     op=ALU.mult,
                 )
+
+        def u_shift(h0, nh):
             r0, r1 = h0 * B, (h0 + nh) * B
             nc.scalar.copy(out=flat[0][:, r0:r1, 4:64], in_=flat[1][:, r0:r1, 0:60])
             nc.scalar.copy(out=flat[2][:, r0:r1, 0:60], in_=flat[1][:, r0:r1, 4:64])
-            for j in (1, 0, 2):
+
+        def u_quant(h0, nh, js):
+            for j in js:
                 nc.vector.quantize_mx(
                     out=uq[j][:, (h0 + 1) * ROW:(h0 + nh + 1) * ROW].bitcast(FP8X4),
                     scales=us[j][:, (h0 + 1) * ROW:(h0 + nh + 1) * ROW],
                     in_=line[j][:, h0 * ROW * 4:(h0 + nh) * ROW * 4],
                 )
 
-        make_u(0, 4)
-        make_u(4, 4)
+        def bias_pe():
+            pb = ps_wt.tile([P, O], F32, tag="wt")
+            nc.tensor.matmul(out=pb[:], lhsT=ones_bf[:], rhs=bias_row[:], start=True, stop=True)
+            return pb
 
-        wq = []
-        ws = []
-        for k in range(NPOS):
+        def bias_out(pb):
+            nc.scalar.copy(
+                out=bias_bc[:].rearrange("p (ot n) -> p ot n", ot=4),
+                in_=pb[:].rearrange("p (n ot) -> p ot n", ot=4),
+            )
+
+        wts = {}
+        wgs = {}
+
+        def w_pe(k, hhs=(0, 1)):
             wf = w_sb[k][:].bitcast(F32)
-            wg = stage.tile([P, 4 * O], BF16, tag="wg", align_bytes=64)
-            wgf = wg[:].bitcast(F32)
-            for hh in range(2):
-                wt = psum.tile([P, 2, 2 * P], F32, tag="ps")
+            for hh in hhs:
+                wt = ps_wt.tile([P, 2, 2 * P], F32, tag="wt")
                 for u in range(2):
                     for o2 in range(2):
                         ot = 2 * hh + o2
@@ -161,95 +186,246 @@ def tile_pvconv2d_kernel(tc, x, Wk, bias, out):
                             wf[:, 256 * ot + P * u:256 * ot + P * u + P],
                             ident[:],
                         )
-                if k < 3 and hh == 1:
-                    nc.vector.tensor_copy(
-                        out=wgf[:, hh * 512:(hh + 1) * 512].rearrange("p (c u) -> p c u", u=2),
-                        in_=wt[:].rearrange("p u c -> p c u"),
-                    )
+                wts[(k, hh)] = wt
+
+        def w_out(k, hh, eng):
+            if hh == 0:
+                wgs[k] = stage.tile([P, 4 * O], BF16, tag="wg", align_bytes=64, name="wg")
+            dst = wgs[k][:].bitcast(F32)[:, hh * 512:(hh + 1) * 512].rearrange("p (c u) -> p c u", u=2)
+            src = wts[(k, hh)][:].rearrange("p u c -> p c u")
+            if eng == "v":
+                nc.vector.tensor_copy(out=dst, in_=src)
+            else:
+                nc.scalar.copy(out=dst, in_=src)
+
+        def w_quant(k):
+            nc.vector.quantize_mx(out=wq[k][:].bitcast(FP8X4), scales=ws[k][:], in_=wgs[k][:])
+
+        accs = {}
+        done = {}
+
+        def mx(T, ks):
+            if T not in accs:
+                if T in (3, 4):
+                    accs[T] = ps_hd.tile([P, O], F32, tag="hd", name="acc_hd")
                 else:
-                    nc.scalar.copy(
-                        out=wgf[:, hh * 512:(hh + 1) * 512].rearrange("p (c u) -> p c u", u=2),
-                        in_=wt[:].rearrange("p u c -> p c u"),
-                    )
-            wqk = big.tile([P, O], U32, name="wq%d" % k, align_bytes=64)
-            wsk = big.tile([P, O], U8, name="ws%d" % k, align_bytes=64)
-            nc.vector.quantize_mx(out=wqk[:].bitcast(FP8X4), scales=wsk[:], in_=wg[:])
-            wq.append(wqk)
-            ws.append(wsk)
+                    accs[T] = ps_acc.tile([P, O], F32, tag="acc", name="acc")
+                done[T] = 0
+            for k in ks:
+                done[T] += 1
+                i, j = divmod(k, 3)
+                c0 = (2 * T + i) * ROW
+                nc.tensor.matmul_mx(
+                    out=accs[T][:],
+                    lhsT=uq[j][:, c0:c0 + P].bitcast(FP8X4),
+                    lhsT_scale=us[j][:, c0:c0 + P],
+                    rhs=wq[k][:].bitcast(FP8X4),
+                    rhs_scale=ws[k][:],
+                    start=(done[T] == 1),
+                    stop=(done[T] == NPOS),
+                )
 
-        make_u(8, 8)
+        tl = {}
 
-        pb = psum.tile([P, O], F32, tag="ps")
-        nc.tensor.matmul(out=pb[:], lhsT=ones_bf[:], rhs=bias_row[:], start=True, stop=True)
-        bias_bc = const.tile([P, O], F32)
-        nc.vector.tensor_copy(
-            out=bias_bc[:].rearrange("p (ot n) -> p ot n", ot=4),
-            in_=pb[:].rearrange("p (n ot) -> p ot n", ot=4),
-        )
-
-        o_sb = big.tile([P, B, 4, HW], F32)
-        out_v = out.rearrange("b (n ot) h w -> b n ot (h w)", ot=4)
-
-        def mx_pass(acc, T, k):
-            i, j = divmod(k, 3)
-            c0 = (2 * T + i) * ROW
-            nc.tensor.matmul_mx(
-                out=acc[:],
-                lhsT=uq[j][:, c0:c0 + P].bitcast(FP8X4),
-                lhsT_scale=us[j][:, c0:c0 + P],
-                rhs=wq[k][:].bitcast(FP8X4),
-                rhs_scale=ws[k][:],
-                start=(k == 0),
-                stop=(k == NPOS - 1),
-            )
-
-        def tail(acc, T):
+        def tail_a(T):
             t_sb = stage.tile([P, O], F32, tag="t")
-            nc.vector.tensor_tensor(out=t_sb[:], in0=acc[:], in1=bias_bc[:], op=ALU.add)
+            nc.vector.tensor_tensor(out=t_sb[:], in0=accs[T][:], in1=bias_bc[:], op=ALU.add)
             sq = stage.tile([P, O], F32, tag="sq")
             m2 = tsmall.tile([P, 1], F32, tag="m2")
             nc.vector.scalar_tensor_tensor(
                 out=sq[:], in0=t_sb[:], scalar=0.0, in1=t_sb[:], op0=ALU.max, op1=ALU.mult, accum_out=m2[:]
             )
-            m2c = tsmall.tile([P, 1], F32, tag="m2c")
-            nc.vector.tensor_scalar(out=m2c[:], in0=m2[:], scalar1=1e-14, scalar2=None, op0=ALU.max)
-            mn = tsmall.tile([P, 1], F32, tag="mn")
-            nc.gpsimd.tensor_tensor(out=mn[:], in0=m2c[:], in1=half[:, 0:1], op=ALU.pow)
+            a2 = tsmall.tile([P, 1], F32, tag="a2")
+            nc.vector.tensor_scalar(out=a2[:], in0=m2[:], scalar1=1e-14, scalar2=0.01, op0=ALU.max, op1=ALU.mult)
+            qv = tsmall.tile([P, 1], F32, tag="qv")
+            nc.gpsimd.tensor_tensor(out=qv[:], in0=a2[:], in1=mhalf[:, 0:1], op=ALU.pow)
+            tl[T] = (t_sb, a2, qv)
+
+        def tail_b(T):
+            t_sb, a2, qv = tl[T]
             th = tsmall.tile([P, 1], F32, tag="th")
-            nc.scalar.activation(out=th[:], in_=mn[:], func=ACT.Tanh, scale=0.1)
-            mr = tsmall.tile([P, 1], F32, tag="mr")
-            nc.vector.reciprocal(out=mr[:], in_=mn[:])
+            nc.scalar.activation(out=th[:], in_=a2[:], func=ACT.Tanh, scale=qv[:, 0:1])
             gs = tsmall.tile([P, 1], F32, tag="gs")
-            nc.vector.scalar_tensor_tensor(
-                out=gs[:], in0=th[:], scalar=10.0, in1=mr[:], op0=ALU.mult, op1=ALU.mult
-            )
+            nc.scalar.activation(out=gs[:], in_=th[:], func=ACT.Copy, scale=qv[:, 0:1])
             rs = stage.tile([P, O], F32, tag="rs")
             nc.scalar.activation(out=rs[:], in_=t_sb[:], func=ACT.Relu, scale=gs[:, 0:1])
-            pt = psum.tile([P, O], F32, tag="ps")
+            tl[T] = rs
+
+        def tail_pe(T):
+            rs = tl[T]
+            pt = ps_wt.tile([P, O], F32, tag="wt")
             for ot in range(4):
                 nc.tensor.transpose(pt[:, ot * P:(ot + 1) * P], rs[:, ot * P:(ot + 1) * P], perm[:])
+            tl[T] = pt
+
+        def tail_c(T, eng="s"):
+            dst = o_sb[:, :, :, 32 * T:32 * T + 32]
+            src = tl[T][:].rearrange("p (ot b q) -> p b ot q", ot=4, b=B)
+            if eng == "v":
+                nc.vector.tensor_copy(out=dst, in_=src)
+            else:
+                nc.scalar.copy(out=dst, in_=src)
+
+        def last_tile(T):
+            t_sb, a2, qv = tl[T]
+            th = tsmall.tile([P, 1], F32, tag="th")
+            nc.scalar.activation(out=th[:], in_=a2[:], func=ACT.Tanh, scale=qv[:, 0:1])
+            gs = tsmall.tile([P, 1], F32, tag="gs")
+            nc.scalar.activation(out=gs[:], in_=th[:], func=ACT.Copy, scale=qv[:, 0:1])
+            rs_a = stage.tile([P, O // 2], F32, tag="rs_a")
+            rs_b = stage.tile([P, O // 2], F32, tag="rs_b")
+            nc.scalar.activation(out=rs_a[:], in_=t_sb[:, 0:256], func=ACT.Relu, scale=gs[:, 0:1])
+            nc.vector.tensor_scalar(
+                out=rs_b[:], in0=t_sb[:, 256:512], scalar1=gs[:, 0:1], scalar2=0.0, op0=ALU.mult, op1=ALU.max
+            )
+            pt_a = ps_wt.tile([P, O // 2], F32, tag="wt")
+            pt_b = ps_wt.tile([P, O // 2], F32, tag="wt")
+            for o2 in range(2):
+                nc.tensor.transpose(pt_a[:, o2 * P:(o2 + 1) * P], rs_a[:, o2 * P:(o2 + 1) * P], perm[:])
+            for o2 in range(2):
+                nc.tensor.transpose(pt_b[:, o2 * P:(o2 + 1) * P], rs_b[:, o2 * P:(o2 + 1) * P], perm[:])
             nc.scalar.copy(
-                out=o_sb[:, :, :, 32 * T:32 * T + 32],
-                in_=pt[:].rearrange("p (ot b q) -> p b ot q", ot=4, b=B),
+                out=o_sb[:, :, 0:2, 32 * T:32 * T + 32],
+                in_=pt_a[:].rearrange("p (ot b q) -> p b ot q", ot=2, b=B),
+            )
+            nc.vector.tensor_copy(
+                out=o_sb[:, :, 2:4, 32 * T:32 * T + 32],
+                in_=pt_b[:].rearrange("p (ot b q) -> p b ot q", ot=2, b=B),
             )
 
         def store(q0, q1):
             for b in range(B):
                 nc.sync.dma_start(out=out_v[b][:, :, q0:q1], in_=o_sb[:, b, :, q0:q1])
 
-        first = [psum.tile([P, O], F32, tag="ps", name="acc%d" % T) for T in range(3)]
-        for k in range(NPOS):
-            for T in range(3):
-                mx_pass(first[T], T, k)
-        for T in range(3):
-            tail(first[T], T)
+        gram_pe(0)
+        gram_pe(1)
+        pb = bias_pe()
+        bias_out(pb)
+        gram_diag(0)
+        c_pow(0)
+        gram_diag(1)
+        c_pow(1)
+        w_pe(0)
+        w_out(0, 0, "s")
+        w_out(0, 1, "v")
+        w_pe(1)
+        c_z(0)
+        c_ln(0)
+        w_quant(0)
+        c_s(0)
+        w_pe(2, (0,))
+        spread(0)
+        w_out(1, 0, "s")
+        c_z(1)
+        c_ln(1)
+        w_out(1, 1, "s")
+        w_pe(2, (1,))
+        c_s(1)
+        spread(1)
+        w_quant(1)
+        w_out(2, 0, "s")
+        w_pe(3, (0,))
+        w_out(2, 1, "s")
+        w_pe(3, (1,))
+        u_mul(0, 2, (0, 1, 2, 3))
+        u_quant(0, 2, (1,))
+        w_out(3, 0, "s")
+        u_shift(0, 2)
+        w_quant(2)
+        w_out(3, 1, "s")
+        u_quant(0, 2, (0, 2))
+        w_pe(4)
+        mx(0, (1, 0, 2))
+        u_mul(2, 2, (0, 1, 2, 3))
+        u_quant(2, 2, (1,))
+        w_out(4, 0, "s")
+        u_shift(2, 2)
+        w_quant(3)
+        w_out(4, 1, "s")
+        u_quant(2, 2, (0, 2))
+        mx(0, (3,))
+        w_pe(5)
+        mx(1, (1, 0, 2, 3))
+        u_mul(4, 4, (0, 1, 2, 3))
+        w_quant(4)
+        u_quant(4, 4, (1,))
+        w_out(5, 0, "s")
+        w_out(5, 1, "s")
+        u_shift(4, 4)
+        mx(0, (4,))
+        mx(1, (4,))
+        w_pe(6)
+        w_quant(5)
+        u_quant(4, 4, (0, 2))
+        w_out(6, 0, "s")
+        w_out(6, 1, "s")
+        mx(0, (5,))
+        mx(1, (5,))
+        mx(2, (1, 4))
+        w_pe(7)
+        mx(2, (0, 2, 3, 5))
+        u_mul(8, 4, (0, 1, 2, 3))
+        w_quant(6)
+        w_out(7, 0, "s")
+        w_out(7, 1, "s")
+        w_pe(8)
+        u_quant(8, 4, (1,))
+        u_shift(8, 4)
+        mx(0, (6,))
+        mx(1, (6,))
+        mx(2, (6,))
+        w_quant(7)
+        w_out(8, 0, "s")
+        w_out(8, 1, "s")
+        u_mul(12, 4, (0, 1, 2, 3))
+        mx(0, (7,))
+        mx(1, (7,))
+        mx(2, (7,))
+        w_quant(8)
+        u_quant(8, 4, (0, 2))
+        u_quant(12, 4, (1,))
+        u_shift(12, 4)
+        mx(0, (8,))
+        mx(1, (8,))
+        mx(2, (8,))
+        tail_a(0)
+        tail_b(0)
+        tail_a(1)
+        tail_b(1)
+        u_quant(12, 4, (0, 2))
+        mx(3, range(9))
+        tail_a(2)
+        tail_b(2)
+        mx(4, range(9))
+        tail_pe(0)
+        tail_pe(1)
+        tail_c(0)
+        tail_c(1)
         store(0, 64)
-        for T in range(3, 8):
-            acc = psum.tile([P, O], F32, tag="ps")
-            for k in range(NPOS):
-                mx_pass(acc, T, k)
-            tail(acc, T)
-            if T in (3, 5):
-                store(32 * (T - 1), 32 * (T + 1))
-            if T in (6, 7):
-                store(32 * T, 32 * (T + 1))
+        tail_a(3)
+        tail_b(3)
+        mx(5, range(9))
+        tail_a(4)
+        tail_b(4)
+        mx(6, range(9))
+        tail_pe(2)
+        tail_pe(3)
+        tail_c(2)
+        tail_c(3)
+        store(64, 128)
+        tail_a(5)
+        tail_b(5)
+        mx(7, range(9))
+        tail_a(6)
+        tail_b(6)
+        tail_pe(4)
+        tail_pe(5)
+        tail_a(7)
+        tail_c(4, "s")
+        tail_c(5, "v")
+        store(128, 192)
+        tail_pe(6)
+        tail_c(6, "s")
+        store(192, 224)
+        last_tile(7)
+        store(224, 256)

@@ -21,6 +21,12 @@ HW = H * W
 ROW = B * W
 NPOS = 9
 FLOPS = 2 * B * HW * C * NPOS * O
+KORD = (1, 0, 2, 4, 3, 5, 7, 6, 8)
+GRAM_BANK = (0, 1, 6, 7)
+W_BANK = (3, 4, 5, 2, 3, 4, 5, 2, 3, 4, 5, 2, 3, 4, 2, 3, 4, 2)
+ACC_BANK = (7, 6, 5, 3, 4, 7, 6, 5)
+PT_BANK = (2, 0, 1, 2, 0, 1, 4, 2, 0)
+LAST_BANK = (5, 3)
 
 
 def tile_pvconv2d_kernel(tc, x, Wk, bias, out):
@@ -31,9 +37,9 @@ def tile_pvconv2d_kernel(tc, x, Wk, bias, out):
         stage = ctx.enter_context(tc.tile_pool(name="stage", bufs=3))
         small = ctx.enter_context(tc.tile_pool(name="small", bufs=1))
         tsmall = ctx.enter_context(tc.tile_pool(name="tsmall", bufs=4))
-        ps_hd = ctx.enter_context(tc.psum_pool(name="ps_hd", bufs=2))
-        ps_wt = ctx.enter_context(tc.psum_pool(name="ps_wt", bufs=3))
-        ps_acc = ctx.enter_context(tc.psum_pool(name="ps_acc", bufs=3))
+        tpool = ctx.enter_context(tc.tile_pool(name="tpool", bufs=4))
+        rpool = ctx.enter_context(tc.tile_pool(name="rpool", bufs=5))
+        psum = ctx.enter_context(tc.psum_pool(name="psum", bufs=1))
         ctx.enter_context(tc.manual_schedule())
 
         x_sb = big.tile([P, B, 4, HW], BF16)
@@ -61,7 +67,7 @@ def tile_pvconv2d_kernel(tc, x, Wk, bias, out):
                 out=x_sb[:, b].rearrange("p (u e) q -> p u (e q)", u=2),
                 in_=x[b].rearrange("(u p e) h w -> p u (e h w)", u=2, e=2),
             )
-        for k in range(NPOS):
+        for k in KORD:
             nc.sync.dma_start(out=w_sb[k][:], in_=Wk[k].rearrange("(n ot) c -> n (ot c)", ot=4))
         make_identity(nc, ident[:])
         nc.gpsimd.memset(half[:], 0.5)
@@ -81,58 +87,62 @@ def tile_pvconv2d_kernel(tc, x, Wk, bias, out):
         nc.vector.memset(g_t[0][:], 0.0)
         nc.vector.memset(g_t[2][:], 0.0)
 
-        n2 = [small.tile([P, 4], F32, name="n2_%d" % g) for g in range(2)]
-        n2c = [small.tile([P, 4], F32, name="n2c_%d" % g) for g in range(2)]
-        nrm = [small.tile([P, 4], F32, name="nrm_%d" % g) for g in range(2)]
-        z = [small.tile([P, 4], F32, name="z_%d" % g) for g in range(2)]
-        l1 = [small.tile([P, 4], F32, name="l1_%d" % g) for g in range(2)]
-        l2 = [small.tile([P, 4], F32, name="l2_%d" % g) for g in range(2)]
-        rec = [small.tile([P, 4], F32, name="rec_%d" % g) for g in range(2)]
-        dl = [small.tile([P, 4], F32, name="dl_%d" % g) for g in range(2)]
-        s = [small.tile([P, 4], F32, name="s_%d" % g) for g in range(2)]
+        def bank(n, shape):
+            return psum.tile(shape, F32, tag="bank%d" % n, name="bank%d" % n)
+
+        n2 = [small.tile([P, 2], F32, name="n2_%d" % b) for b in range(B)]
+        n2c = [small.tile([P, 2], F32, name="n2c_%d" % b) for b in range(B)]
+        nrm = [small.tile([P, 2], F32, name="nrm_%d" % b) for b in range(B)]
+        z = [small.tile([P, 2], F32, name="z_%d" % b) for b in range(B)]
+        l1 = [small.tile([P, 2], F32, name="l1_%d" % b) for b in range(B)]
+        l2 = [small.tile([P, 2], F32, name="l2_%d" % b) for b in range(B)]
+        rec = [small.tile([P, 2], F32, name="rec_%d" % b) for b in range(B)]
+        dl = [small.tile([P, 2], F32, name="dl_%d" % b) for b in range(B)]
+        s = [small.tile([P, 2], F32, name="s_%d" % b) for b in range(B)]
         grams = {}
         sbc = {}
 
-        def gram_pe(g):
-            grams[g] = ps_hd.tile([P, 4, P], F32, tag="hd", name="gram")
-            for mm in range(4):
-                b, hf = divmod(4 * g + mm, 2)
+        def gram_pe(b):
+            grams[b] = bank(GRAM_BANK[b], [P, 2, P])
+            for hf in range(2):
                 for t in range(4):
                     blk = x_sb[:, b, t, hf * P:(hf + 1) * P]
-                    nc.tensor.matmul(out=grams[g][:, mm, :], lhsT=blk, rhs=blk, start=(t == 0), stop=(t == 3))
+                    nc.tensor.matmul(out=grams[b][:, hf, :], lhsT=blk, rhs=blk, start=(t == 0), stop=(t == 3))
 
-        def gram_diag(g):
-            dg = stage.tile([P, 4, P], F32, tag="dg")
+        def gram_diag(b):
+            dg = stage.tile([P, 2, P], F32, tag="dg")
             nc.vector.tensor_tensor(
-                out=dg[:], in0=grams[g][:], in1=ident[:].unsqueeze(1).to_broadcast([P, 4, P]), op=ALU.mult
+                out=dg[:], in0=grams[b][:], in1=ident[:].unsqueeze(1).to_broadcast([P, 2, P]), op=ALU.mult
             )
-            nc.vector.tensor_reduce(out=n2[g][:], in_=dg[:], axis=AX.X, op=ALU.add)
-            nc.vector.tensor_scalar(out=n2c[g][:], in0=n2[g][:], scalar1=1e-14, scalar2=None, op0=ALU.max)
+            nc.vector.tensor_reduce(out=n2[b][:], in_=dg[:], axis=AX.X, op=ALU.add)
+            nc.vector.tensor_scalar(out=n2c[b][:], in0=n2[b][:], scalar1=1e-14, scalar2=None, op0=ALU.max)
 
-        def c_pow(g):
-            nc.gpsimd.tensor_tensor(out=nrm[g][:], in0=n2c[g][:], in1=half[:, 0:4], op=ALU.pow)
+        def c_pow(b):
+            nc.gpsimd.tensor_tensor(out=nrm[b][:], in0=n2c[b][:], in1=half[:, 0:2], op=ALU.pow)
 
-        def c_z(g):
+        def c_z(b):
             nc.vector.tensor_scalar(
-                out=z[g][:], in0=nrm[g][:], scalar1=0.1, scalar2=1.0 - 1e-6, op0=ALU.mult, op1=ALU.min
+                out=z[b][:], in0=nrm[b][:], scalar1=0.1, scalar2=1.0 - 1e-6, op0=ALU.mult, op1=ALU.min
             )
-            nc.vector.reciprocal(out=rec[g][:], in_=nrm[g][:])
+            nc.vector.reciprocal(out=rec[b][:], in_=nrm[b][:])
 
-        def c_ln(g):
-            nc.scalar.activation(out=l1[g][:], in_=z[g][:], func=ACT.Ln, bias=1.0, scale=1.0)
-            nc.scalar.activation(out=l2[g][:], in_=z[g][:], func=ACT.Ln, bias=1.0, scale=-1.0)
+        def c_ln(b):
+            nc.scalar.activation(out=l1[b][:], in_=z[b][:], func=ACT.Ln, bias=1.0, scale=1.0)
+            nc.scalar.activation(out=l2[b][:], in_=z[b][:], func=ACT.Ln, bias=1.0, scale=-1.0)
 
-        def c_s(g):
-            nc.vector.tensor_tensor(out=dl[g][:], in0=l1[g][:], in1=l2[g][:], op=ALU.subtract)
+        def c_s(b):
+            nc.vector.tensor_tensor(out=dl[b][:], in0=l1[b][:], in1=l2[b][:], op=ALU.subtract)
             nc.vector.scalar_tensor_tensor(
-                out=s[g][:], in0=dl[g][:], scalar=5.0, in1=rec[g][:], op0=ALU.mult, op1=ALU.mult
+                out=s[b][:], in0=dl[b][:], scalar=5.0, in1=rec[b][:], op0=ALU.mult, op1=ALU.mult
             )
 
         def spread(g):
-            sbc[g] = ps_hd.tile([P, 4 * P], F32, tag="hd", name="sbc")
+            sbc[g] = bank(g, [P, 4 * P])
             for mm in range(4):
                 nc.tensor.transpose(
-                    sbc[g][:, mm * P:(mm + 1) * P], s[g][:, mm:mm + 1].to_broadcast([P, P]), ident[:]
+                    sbc[g][:, mm * P:(mm + 1) * P],
+                    s[2 * g + mm // 2][:, mm % 2:mm % 2 + 1].to_broadcast([P, P]),
+                    ident[:],
                 )
 
         def u_mul(h0, nh, bs):
@@ -161,7 +171,7 @@ def tile_pvconv2d_kernel(tc, x, Wk, bias, out):
                 )
 
         def bias_pe():
-            pb = ps_wt.tile([P, O], F32, tag="wt")
+            pb = bank(2, [P, O])
             nc.tensor.matmul(out=pb[:], lhsT=ones_bf[:], rhs=bias_row[:], start=True, stop=True)
             return pb
 
@@ -174,10 +184,11 @@ def tile_pvconv2d_kernel(tc, x, Wk, bias, out):
         wts = {}
         wgs = {}
 
-        def w_pe(k, hhs=(0, 1)):
+        def w_pe(n, hhs=(0, 1)):
+            k = KORD[n]
             wf = w_sb[k][:].bitcast(F32)
             for hh in hhs:
-                wt = ps_wt.tile([P, 2, 2 * P], F32, tag="wt")
+                wt = bank(W_BANK[2 * n + hh], [P, 2, 2 * P])
                 for u in range(2):
                     for o2 in range(2):
                         ot = 2 * hh + o2
@@ -188,7 +199,8 @@ def tile_pvconv2d_kernel(tc, x, Wk, bias, out):
                         )
                 wts[(k, hh)] = wt
 
-        def w_out(k, hh, eng):
+        def w_out(n, hh, eng):
+            k = KORD[n]
             if hh == 0:
                 wgs[k] = stage.tile([P, 4 * O], BF16, tag="wg", align_bytes=64, name="wg")
             dst = wgs[k][:].bitcast(F32)[:, hh * 512:(hh + 1) * 512].rearrange("p (c u) -> p c u", u=2)
@@ -198,7 +210,8 @@ def tile_pvconv2d_kernel(tc, x, Wk, bias, out):
             else:
                 nc.scalar.copy(out=dst, in_=src)
 
-        def w_quant(k):
+        def w_quant(n):
+            k = KORD[n]
             nc.vector.quantize_mx(out=wq[k][:].bitcast(FP8X4), scales=ws[k][:], in_=wgs[k][:])
 
         accs = {}
@@ -206,10 +219,7 @@ def tile_pvconv2d_kernel(tc, x, Wk, bias, out):
 
         def mx(T, ks):
             if T not in accs:
-                if T in (3, 4):
-                    accs[T] = ps_hd.tile([P, O], F32, tag="hd", name="acc_hd")
-                else:
-                    accs[T] = ps_acc.tile([P, O], F32, tag="acc", name="acc")
+                accs[T] = bank(ACC_BANK[T], [P, O])
                 done[T] = 0
             for k in ks:
                 done[T] += 1
@@ -227,9 +237,17 @@ def tile_pvconv2d_kernel(tc, x, Wk, bias, out):
 
         tl = {}
 
-        def tail_a(T):
-            t_sb = stage.tile([P, O], F32, tag="t")
+        def tail_add(T):
+            t_sb = tpool.tile([P, O], F32, tag="t")
             nc.vector.tensor_tensor(out=t_sb[:], in0=accs[T][:], in1=bias_bc[:], op=ALU.add)
+            tl[T] = t_sb
+
+        def tail_a(T):
+            tail_add(T)
+            tail_ss(T)
+
+        def tail_ss(T):
+            t_sb = tl[T]
             sq = stage.tile([P, O], F32, tag="sq")
             m2 = tsmall.tile([P, 1], F32, tag="m2")
             nc.vector.scalar_tensor_tensor(
@@ -247,13 +265,13 @@ def tile_pvconv2d_kernel(tc, x, Wk, bias, out):
             nc.scalar.activation(out=th[:], in_=a2[:], func=ACT.Tanh, scale=qv[:, 0:1])
             gs = tsmall.tile([P, 1], F32, tag="gs")
             nc.scalar.activation(out=gs[:], in_=th[:], func=ACT.Copy, scale=qv[:, 0:1])
-            rs = stage.tile([P, O], F32, tag="rs")
+            rs = rpool.tile([P, O], F32, tag="rs")
             nc.scalar.activation(out=rs[:], in_=t_sb[:], func=ACT.Relu, scale=gs[:, 0:1])
             tl[T] = rs
 
         def tail_pe(T):
             rs = tl[T]
-            pt = ps_wt.tile([P, O], F32, tag="wt")
+            pt = bank(PT_BANK[T], [P, O])
             for ot in range(4):
                 nc.tensor.transpose(pt[:, ot * P:(ot + 1) * P], rs[:, ot * P:(ot + 1) * P], perm[:])
             tl[T] = pt
@@ -265,6 +283,45 @@ def tile_pvconv2d_kernel(tc, x, Wk, bias, out):
                 nc.vector.tensor_copy(out=dst, in_=src)
             else:
                 nc.scalar.copy(out=dst, in_=src)
+
+        lacc = {}
+        lm2 = {}
+
+        def last_mx(T, hf):
+            lacc[hf] = bank(LAST_BANK[hf], [P, O // 2])
+            for n, k in enumerate(KORD):
+                i, j = divmod(k, 3)
+                c0 = (2 * T + i) * ROW
+                nc.tensor.matmul_mx(
+                    out=lacc[hf][:],
+                    lhsT=uq[j][:, c0:c0 + P].bitcast(FP8X4),
+                    lhsT_scale=us[j][:, c0:c0 + P],
+                    rhs=wq[k][:, hf * 256:(hf + 1) * 256].bitcast(FP8X4),
+                    rhs_scale=ws[k][:, hf * 256:(hf + 1) * 256],
+                    start=(n == 0),
+                    stop=(n == NPOS - 1),
+                )
+
+        def last_a(T, hf):
+            if hf == 0:
+                tl[T] = tpool.tile([P, O], F32, tag="t", name="t_last")
+            cols = slice(hf * 256, (hf + 1) * 256)
+            nc.vector.tensor_tensor(out=tl[T][:, cols], in0=lacc[hf][:], in1=bias_bc[:, cols], op=ALU.add)
+            sq = stage.tile([P, O // 2], F32, tag="sq")
+            lm2[hf] = tsmall.tile([P, 1], F32, tag="lm2_%d" % hf, name="lm2")
+            nc.vector.scalar_tensor_tensor(
+                out=sq[:], in0=tl[T][:, cols], scalar=0.0, in1=tl[T][:, cols], op0=ALU.max, op1=ALU.mult,
+                accum_out=lm2[hf][:],
+            )
+
+        def last_m(T):
+            m2 = tsmall.tile([P, 1], F32, tag="m2")
+            nc.vector.tensor_tensor(out=m2[:], in0=lm2[0][:], in1=lm2[1][:], op=ALU.add)
+            a2 = tsmall.tile([P, 1], F32, tag="a2")
+            nc.vector.tensor_scalar(out=a2[:], in0=m2[:], scalar1=1e-14, scalar2=0.01, op0=ALU.max, op1=ALU.mult)
+            qv = tsmall.tile([P, 1], F32, tag="qv")
+            nc.gpsimd.tensor_tensor(out=qv[:], in0=a2[:], in1=mhalf[:, 0:1], op=ALU.pow)
+            tl[T] = (tl[T], a2, qv)
 
         def last_tile(T):
             t_sb, a2, qv = tl[T]
@@ -278,8 +335,8 @@ def tile_pvconv2d_kernel(tc, x, Wk, bias, out):
             nc.vector.tensor_scalar(
                 out=rs_b[:], in0=t_sb[:, 256:512], scalar1=gs[:, 0:1], scalar2=0.0, op0=ALU.mult, op1=ALU.max
             )
-            pt_a = ps_wt.tile([P, O // 2], F32, tag="wt")
-            pt_b = ps_wt.tile([P, O // 2], F32, tag="wt")
+            pt_a = bank(PT_BANK[T], [P, O // 2])
+            pt_b = bank(PT_BANK[T + 1], [P, O // 2])
             for o2 in range(2):
                 nc.tensor.transpose(pt_a[:, o2 * P:(o2 + 1) * P], rs_a[:, o2 * P:(o2 + 1) * P], perm[:])
             for o2 in range(2):
@@ -298,133 +355,153 @@ def tile_pvconv2d_kernel(tc, x, Wk, bias, out):
                 nc.sync.dma_start(out=out_v[b][:, :, q0:q1], in_=o_sb[:, b, :, q0:q1])
 
         gram_pe(0)
-        gram_pe(1)
-        pb = bias_pe()
-        bias_out(pb)
         gram_diag(0)
         c_pow(0)
+        gram_pe(1)
         gram_diag(1)
         c_pow(1)
-        w_pe(0)
-        w_out(0, 0, "s")
-        w_out(0, 1, "v")
-        w_pe(1)
+        gram_pe(2)
+        gram_diag(2)
+        c_pow(2)
+        gram_pe(3)
+        pb = bias_pe()
+        bias_out(pb)
         c_z(0)
         c_ln(0)
-        w_quant(0)
-        c_s(0)
-        w_pe(2, (0,))
-        spread(0)
-        w_out(1, 0, "s")
+        gram_diag(3)
+        c_pow(3)
+        w_pe(0)
+        w_out(0, 0, "s")
         c_z(1)
         c_ln(1)
+        c_s(0)
+        c_z(2)
+        w_out(0, 1, "s")
+        c_ln(2)
+        c_s(1)
+        w_pe(1)
+        spread(0)
+        c_z(3)
+        c_ln(3)
+        c_s(2)
+        w_quant(0)
+        c_s(3)
+        w_pe(2, (0,))
+        spread(1)
+        w_out(1, 0, "s")
         w_out(1, 1, "s")
         w_pe(2, (1,))
-        c_s(1)
-        spread(1)
-        w_quant(1)
-        w_out(2, 0, "s")
-        w_pe(3, (0,))
-        w_out(2, 1, "s")
-        w_pe(3, (1,))
         u_mul(0, 2, (0, 1, 2, 3))
         u_quant(0, 2, (1,))
-        w_out(3, 0, "s")
+        w_quant(1)
+        w_out(2, 0, "s")
+        w_out(2, 1, "s")
+        w_pe(3)
         u_shift(0, 2)
-        w_quant(2)
-        w_out(3, 1, "s")
+        mx(0, (1,))
         u_quant(0, 2, (0, 2))
         w_pe(4)
-        mx(0, (1, 0, 2))
         u_mul(2, 2, (0, 1, 2, 3))
-        u_quant(2, 2, (1,))
-        w_out(4, 0, "s")
-        u_shift(2, 2)
-        w_quant(3)
-        w_out(4, 1, "s")
-        u_quant(2, 2, (0, 2))
-        mx(0, (3,))
+        w_quant(2)
+        w_out(3, 0, "s")
+        w_out(3, 1, "s")
+        mx(0, (0,))
         w_pe(5)
-        mx(1, (1, 0, 2, 3))
+        u_quant(2, 2, (1,))
+        u_shift(2, 2)
+        u_quant(2, 2, (0, 2))
+        mx(0, (2,))
+        mx(1, (1, 0, 2))
+        w_quant(3)
+        w_out(4, 0, "s")
+        w_out(4, 1, "s")
+        w_pe(6)
         u_mul(4, 4, (0, 1, 2, 3))
-        w_quant(4)
         u_quant(4, 4, (1,))
         w_out(5, 0, "s")
         w_out(5, 1, "s")
-        u_shift(4, 4)
         mx(0, (4,))
         mx(1, (4,))
-        w_pe(6)
-        w_quant(5)
-        u_quant(4, 4, (0, 2))
+        w_quant(4)
         w_out(6, 0, "s")
         w_out(6, 1, "s")
+        w_pe(7)
+        u_shift(4, 4)
+        u_quant(4, 4, (0, 2))
+        mx(0, (3,))
+        mx(1, (3,))
+        mx(2, (1, 4, 0, 2, 3))
+        w_quant(5)
+        w_out(7, 0, "s")
+        w_pe(8)
+        w_out(7, 1, "s")
+        w_quant(6)
         mx(0, (5,))
         mx(1, (5,))
-        mx(2, (1, 4))
-        w_pe(7)
-        mx(2, (0, 2, 3, 5))
+        mx(2, (5,))
         u_mul(8, 4, (0, 1, 2, 3))
-        w_quant(6)
-        w_out(7, 0, "s")
-        w_out(7, 1, "s")
-        w_pe(8)
-        u_quant(8, 4, (1,))
-        u_shift(8, 4)
-        mx(0, (6,))
-        mx(1, (6,))
-        mx(2, (6,))
-        w_quant(7)
         w_out(8, 0, "s")
         w_out(8, 1, "s")
-        u_mul(12, 4, (0, 1, 2, 3))
+        w_quant(7)
         mx(0, (7,))
         mx(1, (7,))
         mx(2, (7,))
+        u_quant(8, 4, (1,))
+        u_shift(8, 4)
         w_quant(8)
+        mx(0, (6,))
+        mx(1, (6,))
+        mx(2, (6,))
         u_quant(8, 4, (0, 2))
-        u_quant(12, 4, (1,))
-        u_shift(12, 4)
         mx(0, (8,))
         mx(1, (8,))
         mx(2, (8,))
-        tail_a(0)
+        tail_add(0)
+        mx(3, (1, 4, 0, 2, 3, 5, 7, 6, 8))
+        tail_add(1)
+        tail_ss(0)
         tail_b(0)
-        tail_a(1)
+        tail_add(2)
+        tail_ss(1)
         tail_b(1)
-        u_quant(12, 4, (0, 2))
-        mx(3, range(9))
-        tail_a(2)
+        tail_ss(2)
         tail_b(2)
+        u_mul(12, 4, (0, 1, 2, 3))
+        u_quant(12, 4, (1,))
+        u_shift(12, 4)
+        tail_a(3)
+        u_quant(12, 4, (0, 2))
+        tail_b(3)
         mx(4, range(9))
         tail_pe(0)
         tail_pe(1)
+        tail_a(4)
         tail_c(0)
         tail_c(1)
         store(0, 64)
-        tail_a(3)
-        tail_b(3)
-        mx(5, range(9))
-        tail_a(4)
         tail_b(4)
-        mx(6, range(9))
+        mx(5, range(9))
         tail_pe(2)
         tail_pe(3)
+        tail_a(5)
         tail_c(2)
         tail_c(3)
         store(64, 128)
-        tail_a(5)
         tail_b(5)
-        mx(7, range(9))
-        tail_a(6)
-        tail_b(6)
+        mx(6, range(9))
         tail_pe(4)
         tail_pe(5)
-        tail_a(7)
-        tail_c(4, "s")
-        tail_c(5, "v")
+        tail_a(6)
+        tail_c(4)
+        tail_c(5)
         store(128, 192)
+        tail_b(6)
+        last_mx(7, 0)
+        last_mx(7, 1)
+        last_a(7, 0)
         tail_pe(6)
+        last_a(7, 1)
+        last_m(7)
         tail_c(6, "s")
         store(192, 224)
         last_tile(7)

@@ -21,6 +21,7 @@ HW = H * W
 ROW = B * W
 NPOS = 9
 FLOPS = 2 * B * HW * C * NPOS * O
+ZMAX = 1.0 - 1e-6
 KORD = (1, 0, 2, 4, 3, 5, 7, 6, 8)
 GRAM_BANK = (0, 1, 6, 7)
 W_BANK = (3, 4, 5, 2, 3, 4, 5, 2, 3, 4, 5, 2, 3, 4, 2, 3, 4, 2)
@@ -53,7 +54,6 @@ def tile_pvconv2d_kernel(tc, x, Wk, bias, out):
         out_v = out.rearrange("b (n ot) h w -> b n ot (h w)", ot=4)
         ident = const.tile([P, P], F32)
         perm = const.tile([P, P], F32)
-        half = const.tile([P, 8], F32)
         mhalf = const.tile([P, 8], F32)
         ones_bf = const.tile([P, P], BF16)
         bias_row = const.tile([P, O], BF16)
@@ -70,7 +70,6 @@ def tile_pvconv2d_kernel(tc, x, Wk, bias, out):
         for k in KORD:
             nc.sync.dma_start(out=w_sb[k][:], in_=Wk[k].rearrange("(n ot) c -> n (ot c)", ot=4))
         make_identity(nc, ident[:])
-        nc.gpsimd.memset(half[:], 0.5)
         nc.gpsimd.memset(mhalf[:], -0.5)
         nc.gpsimd.memset(bias_row[:], 0.0)
         nc.scalar.dma_start(out=bias_row[0:1, :], in_=bias.unsqueeze(0))
@@ -79,7 +78,7 @@ def tile_pvconv2d_kernel(tc, x, Wk, bias, out):
             out=perm[:].rearrange("p (b hh w) -> p b hh w", b=B, hh=2),
             in_=ident[:].rearrange("p (hh b w) -> p b hh w", hh=2, b=B),
         )
-        nc.scalar.activation(out=junk[:], in_=half[:], func=ACT.Ln)
+        nc.scalar.activation(out=junk[:], in_=mhalf[:], func=ACT.Sqrt, scale=-1.0)
         for j in range(3):
             nc.vector.memset(us[j][:].bitcast(I32), 0)
             nc.vector.memset(uq[j][:, 0:ROW].bitcast(I32), 0)
@@ -90,15 +89,15 @@ def tile_pvconv2d_kernel(tc, x, Wk, bias, out):
         def bank(n, shape):
             return psum.tile(shape, F32, tag="bank%d" % n, name="bank%d" % n)
 
-        n2 = [small.tile([P, 2], F32, name="n2_%d" % b) for b in range(B)]
-        n2c = [small.tile([P, 2], F32, name="n2c_%d" % b) for b in range(B)]
-        nrm = [small.tile([P, 2], F32, name="nrm_%d" % b) for b in range(B)]
-        z = [small.tile([P, 2], F32, name="z_%d" % b) for b in range(B)]
-        l1 = [small.tile([P, 2], F32, name="l1_%d" % b) for b in range(B)]
-        l2 = [small.tile([P, 2], F32, name="l2_%d" % b) for b in range(B)]
-        rec = [small.tile([P, 2], F32, name="rec_%d" % b) for b in range(B)]
-        dl = [small.tile([P, 2], F32, name="dl_%d" % b) for b in range(B)]
-        s = [small.tile([P, 2], F32, name="s_%d" % b) for b in range(B)]
+        n2 = small.tile([P, 8], F32)
+        n2c = small.tile([P, 8], F32)
+        y = small.tile([P, 8], F32)
+        r1 = small.tile([P, 8], F32)
+        l1 = small.tile([P, 8], F32)
+        l2 = small.tile([P, 8], F32)
+        rec = small.tile([P, 8], F32)
+        dl = small.tile([P, 8], F32)
+        s = small.tile([P, 8], F32)
         grams = {}
         sbc = {}
 
@@ -114,26 +113,24 @@ def tile_pvconv2d_kernel(tc, x, Wk, bias, out):
             nc.vector.tensor_tensor(
                 out=dg[:], in0=grams[b][:], in1=ident[:].unsqueeze(1).to_broadcast([P, 2, P]), op=ALU.mult
             )
-            nc.vector.tensor_reduce(out=n2[b][:], in_=dg[:], axis=AX.X, op=ALU.add)
-            nc.vector.tensor_scalar(out=n2c[b][:], in0=n2[b][:], scalar1=1e-14, scalar2=None, op0=ALU.max)
+            nc.vector.tensor_reduce(out=n2[:, 2 * b:2 * b + 2], in_=dg[:], axis=AX.X, op=ALU.add)
 
-        def c_pow(b):
-            nc.gpsimd.tensor_tensor(out=nrm[b][:], in0=n2c[b][:], in1=half[:, 0:2], op=ALU.pow)
+        def c_root():
+            nc.vector.tensor_scalar(out=n2c[:], in0=n2[:], scalar1=1e-14, scalar2=None, op0=ALU.max)
+            nc.scalar.activation(out=y[:], in_=n2c[:], func=ACT.Sqrt, scale=0.01)
+            nc.scalar.activation(out=r1[:], in_=y[:], func=ACT.Relu, bias=ZMAX, scale=-1.0)
 
-        def c_z(b):
-            nc.vector.tensor_scalar(
-                out=z[b][:], in0=nrm[b][:], scalar1=0.1, scalar2=1.0 - 1e-6, op0=ALU.mult, op1=ALU.min
-            )
-            nc.vector.reciprocal(out=rec[b][:], in_=nrm[b][:])
+        def c_ln():
+            nc.scalar.activation(out=l1[:], in_=r1[:], func=ACT.Ln, bias=1.0 + ZMAX, scale=-1.0)
+            nc.scalar.activation(out=l2[:], in_=r1[:], func=ACT.Ln, bias=1.0 - ZMAX, scale=1.0)
 
-        def c_ln(b):
-            nc.scalar.activation(out=l1[b][:], in_=z[b][:], func=ACT.Ln, bias=1.0, scale=1.0)
-            nc.scalar.activation(out=l2[b][:], in_=z[b][:], func=ACT.Ln, bias=1.0, scale=-1.0)
+        def c_rec():
+            nc.vector.reciprocal(out=rec[:], in_=y[:])
 
-        def c_s(b):
-            nc.vector.tensor_tensor(out=dl[b][:], in0=l1[b][:], in1=l2[b][:], op=ALU.subtract)
+        def c_s():
+            nc.vector.tensor_tensor(out=dl[:], in0=l1[:], in1=l2[:], op=ALU.subtract)
             nc.vector.scalar_tensor_tensor(
-                out=s[b][:], in0=dl[b][:], scalar=5.0, in1=rec[b][:], op0=ALU.mult, op1=ALU.mult
+                out=s[:], in0=dl[:], scalar=0.5, in1=rec[:], op0=ALU.mult, op1=ALU.mult
             )
 
         def spread(g):
@@ -141,7 +138,7 @@ def tile_pvconv2d_kernel(tc, x, Wk, bias, out):
             for mm in range(4):
                 nc.tensor.transpose(
                     sbc[g][:, mm * P:(mm + 1) * P],
-                    s[2 * g + mm // 2][:, mm % 2:mm % 2 + 1].to_broadcast([P, P]),
+                    s[:, 4 * g + mm:4 * g + mm + 1].to_broadcast([P, P]),
                     ident[:],
                 )
 
@@ -253,20 +250,32 @@ def tile_pvconv2d_kernel(tc, x, Wk, bias, out):
             nc.vector.scalar_tensor_tensor(
                 out=sq[:], in0=t_sb[:], scalar=0.0, in1=t_sb[:], op0=ALU.max, op1=ALU.mult, accum_out=m2[:]
             )
+            tail_q(T, t_sb, m2, ACT.Relu)
+
+        def tail_ss_s(T):
+            t_sb = tl[T]
+            r_sb = tpool.tile([P, O], F32, tag="r")
+            nc.scalar.activation(out=r_sb[:], in_=t_sb[:], func=ACT.Relu)
+            sq = stage.tile([P, O], F32, tag="sq_s")
+            m2 = tsmall.tile([P, 1], F32, tag="m2")
+            nc.scalar.activation(out=sq[:], in_=r_sb[:], func=ACT.Square, accum_out=m2[:])
+            tail_q(T, r_sb, m2, ACT.Copy)
+
+        def tail_q(T, src, m2, func):
             a2 = tsmall.tile([P, 1], F32, tag="a2")
-            nc.vector.tensor_scalar(out=a2[:], in0=m2[:], scalar1=1e-14, scalar2=0.01, op0=ALU.max, op1=ALU.mult)
+            nc.gpsimd.tensor_scalar(out=a2[:], in0=m2[:], scalar1=1e-14, scalar2=0.01, op0=ALU.max, op1=ALU.mult)
             qv = tsmall.tile([P, 1], F32, tag="qv")
             nc.gpsimd.tensor_tensor(out=qv[:], in0=a2[:], in1=mhalf[:, 0:1], op=ALU.pow)
-            tl[T] = (t_sb, a2, qv)
+            tl[T] = (src, a2, qv, func)
 
         def tail_b(T):
-            t_sb, a2, qv = tl[T]
+            t_sb, a2, qv, func = tl[T]
             th = tsmall.tile([P, 1], F32, tag="th")
             nc.scalar.activation(out=th[:], in_=a2[:], func=ACT.Tanh, scale=qv[:, 0:1])
             gs = tsmall.tile([P, 1], F32, tag="gs")
             nc.scalar.activation(out=gs[:], in_=th[:], func=ACT.Copy, scale=qv[:, 0:1])
             rs = rpool.tile([P, O], F32, tag="rs")
-            nc.scalar.activation(out=rs[:], in_=t_sb[:], func=ACT.Relu, scale=gs[:, 0:1])
+            nc.scalar.activation(out=rs[:], in_=t_sb[:], func=func, scale=gs[:, 0:1])
             tl[T] = rs
 
         def tail_pe(T):
@@ -356,37 +365,25 @@ def tile_pvconv2d_kernel(tc, x, Wk, bias, out):
 
         gram_pe(0)
         gram_diag(0)
-        c_pow(0)
         gram_pe(1)
         gram_diag(1)
-        c_pow(1)
         gram_pe(2)
         gram_diag(2)
-        c_pow(2)
         gram_pe(3)
         pb = bias_pe()
         bias_out(pb)
-        c_z(0)
-        c_ln(0)
         gram_diag(3)
-        c_pow(3)
+        c_root()
+        c_ln()
         w_pe(0)
-        w_out(0, 0, "s")
-        c_z(1)
-        c_ln(1)
-        c_s(0)
-        c_z(2)
-        w_out(0, 1, "s")
-        c_ln(2)
-        c_s(1)
+        w_out(0, 0, "v")
+        c_rec()
+        w_out(0, 1, "v")
         w_pe(1)
-        spread(0)
-        c_z(3)
-        c_ln(3)
-        c_s(2)
         w_quant(0)
-        c_s(3)
+        c_s()
         w_pe(2, (0,))
+        spread(0)
         spread(1)
         w_out(1, 0, "s")
         w_out(1, 1, "s")
@@ -458,50 +455,50 @@ def tile_pvconv2d_kernel(tc, x, Wk, bias, out):
         mx(2, (8,))
         tail_add(0)
         mx(3, (1, 4, 0, 2, 3, 5, 7, 6, 8))
+        tail_ss_s(0)
         tail_add(1)
-        tail_ss(0)
-        tail_b(0)
+        tail_ss_s(1)
         tail_add(2)
-        tail_ss(1)
-        tail_b(1)
-        tail_ss(2)
-        tail_b(2)
+        tail_ss_s(2)
         u_mul(12, 4, (0, 1, 2, 3))
         u_quant(12, 4, (1,))
         u_shift(12, 4)
-        tail_a(3)
+        tail_b(0)
         u_quant(12, 4, (0, 2))
+        tail_b(1)
+        tail_a(3)
+        tail_b(2)
         tail_b(3)
         mx(4, range(9))
+        tail_a(4)
+        tail_b(4)
+        mx(5, range(9))
         tail_pe(0)
         tail_pe(1)
-        tail_a(4)
+        tail_a(5)
         tail_c(0)
         tail_c(1)
         store(0, 64)
-        tail_b(4)
-        mx(5, range(9))
+        tail_b(5)
+        mx(6, range(9))
         tail_pe(2)
         tail_pe(3)
-        tail_a(5)
+        tail_pe(4)
+        tail_a(6)
         tail_c(2)
         tail_c(3)
         store(64, 128)
-        tail_b(5)
-        mx(6, range(9))
-        tail_pe(4)
-        tail_pe(5)
-        tail_a(6)
         tail_c(4)
-        tail_c(5)
-        store(128, 192)
         tail_b(6)
         last_mx(7, 0)
         last_mx(7, 1)
         last_a(7, 0)
+        tail_pe(5)
         tail_pe(6)
         last_a(7, 1)
         last_m(7)
+        tail_c(5, "s")
+        store(128, 192)
         tail_c(6, "s")
         store(192, 224)
         last_tile(7)

@@ -21,13 +21,6 @@ HW = H * W
 ROW = B * W
 NPOS = 9
 FLOPS = 2 * B * HW * C * NPOS * O
-ZMAX = 1.0 - 1e-6
-KORD = (1, 0, 2, 4, 3, 5, 7, 6, 8)
-GRAM_BANK = (0, 1, 6, 7)
-W_BANK = (3, 4, 5, 2, 3, 4, 5, 2, 3, 4, 5, 2, 3, 4, 2, 3, 4, 2)
-ACC_BANK = (7, 6, 5, 3, 4, 7, 6, 5)
-PT_BANK = (2, 0, 1, 2, 0, 1, 4, 2, 0)
-LAST_BANK = (5, 3)
 
 
 def tile_pvconv2d_kernel(tc, x, Wk, bias, out):
@@ -38,10 +31,9 @@ def tile_pvconv2d_kernel(tc, x, Wk, bias, out):
         stage = ctx.enter_context(tc.tile_pool(name="stage", bufs=3))
         small = ctx.enter_context(tc.tile_pool(name="small", bufs=1))
         tsmall = ctx.enter_context(tc.tile_pool(name="tsmall", bufs=4))
-        tpool = ctx.enter_context(tc.tile_pool(name="tpool", bufs=4))
-        rpool = ctx.enter_context(tc.tile_pool(name="rpool", bufs=5))
-        psum = ctx.enter_context(tc.psum_pool(name="psum", bufs=1))
-        ctx.enter_context(tc.manual_schedule())
+        ps_hd = ctx.enter_context(tc.psum_pool(name="ps_hd", bufs=2))
+        ps_wt = ctx.enter_context(tc.psum_pool(name="ps_wt", bufs=3))
+        ps_acc = ctx.enter_context(tc.psum_pool(name="ps_acc", bufs=3))
 
         x_sb = big.tile([P, B, 4, HW], BF16)
         w_sb = [big.tile([P, 4 * C], BF16, name="w_sb%d" % k) for k in range(NPOS)]
@@ -54,6 +46,7 @@ def tile_pvconv2d_kernel(tc, x, Wk, bias, out):
         out_v = out.rearrange("b (n ot) h w -> b n ot (h w)", ot=4)
         ident = const.tile([P, P], F32)
         perm = const.tile([P, P], F32)
+        half = const.tile([P, 8], F32)
         mhalf = const.tile([P, 8], F32)
         ones_bf = const.tile([P, P], BF16)
         bias_row = const.tile([P, O], BF16)
@@ -67,9 +60,10 @@ def tile_pvconv2d_kernel(tc, x, Wk, bias, out):
                 out=x_sb[:, b].rearrange("p (u e) q -> p u (e q)", u=2),
                 in_=x[b].rearrange("(u p e) h w -> p u (e h w)", u=2, e=2),
             )
-        for k in KORD:
+        for k in range(NPOS):
             nc.sync.dma_start(out=w_sb[k][:], in_=Wk[k].rearrange("(n ot) c -> n (ot c)", ot=4))
         make_identity(nc, ident[:])
+        nc.gpsimd.memset(half[:], 0.5)
         nc.gpsimd.memset(mhalf[:], -0.5)
         nc.gpsimd.memset(bias_row[:], 0.0)
         nc.scalar.dma_start(out=bias_row[0:1, :], in_=bias.unsqueeze(0))
@@ -78,7 +72,7 @@ def tile_pvconv2d_kernel(tc, x, Wk, bias, out):
             out=perm[:].rearrange("p (b hh w) -> p b hh w", b=B, hh=2),
             in_=ident[:].rearrange("p (hh b w) -> p b hh w", hh=2, b=B),
         )
-        nc.scalar.activation(out=junk[:], in_=mhalf[:], func=ACT.Sqrt, scale=-1.0)
+        nc.scalar.activation(out=junk[:], in_=half[:], func=ACT.Ln)
         for j in range(3):
             nc.vector.memset(us[j][:].bitcast(I32), 0)
             nc.vector.memset(uq[j][:, 0:ROW].bitcast(I32), 0)
@@ -86,60 +80,58 @@ def tile_pvconv2d_kernel(tc, x, Wk, bias, out):
         nc.vector.memset(g_t[0][:], 0.0)
         nc.vector.memset(g_t[2][:], 0.0)
 
-        def bank(n, shape):
-            return psum.tile(shape, F32, tag="bank%d" % n, name="bank%d" % n)
-
-        n2 = small.tile([P, 8], F32)
-        n2c = small.tile([P, 8], F32)
-        y = small.tile([P, 8], F32)
-        r1 = small.tile([P, 8], F32)
-        l1 = small.tile([P, 8], F32)
-        l2 = small.tile([P, 8], F32)
-        rec = small.tile([P, 8], F32)
-        dl = small.tile([P, 8], F32)
-        s = small.tile([P, 8], F32)
+        n2 = [small.tile([P, 4], F32, name="n2_%d" % g) for g in range(2)]
+        n2c = [small.tile([P, 4], F32, name="n2c_%d" % g) for g in range(2)]
+        nrm = [small.tile([P, 4], F32, name="nrm_%d" % g) for g in range(2)]
+        z = [small.tile([P, 4], F32, name="z_%d" % g) for g in range(2)]
+        l1 = [small.tile([P, 4], F32, name="l1_%d" % g) for g in range(2)]
+        l2 = [small.tile([P, 4], F32, name="l2_%d" % g) for g in range(2)]
+        rec = [small.tile([P, 4], F32, name="rec_%d" % g) for g in range(2)]
+        dl = [small.tile([P, 4], F32, name="dl_%d" % g) for g in range(2)]
+        s = [small.tile([P, 4], F32, name="s_%d" % g) for g in range(2)]
         grams = {}
         sbc = {}
 
-        def gram_pe(b):
-            grams[b] = bank(GRAM_BANK[b], [P, 2, P])
-            for hf in range(2):
+        def gram_pe(g):
+            grams[g] = ps_hd.tile([P, 4, P], F32, tag="hd", name="gram")
+            for mm in range(4):
+                b, hf = divmod(4 * g + mm, 2)
                 for t in range(4):
                     blk = x_sb[:, b, t, hf * P:(hf + 1) * P]
-                    nc.tensor.matmul(out=grams[b][:, hf, :], lhsT=blk, rhs=blk, start=(t == 0), stop=(t == 3))
+                    nc.tensor.matmul(out=grams[g][:, mm, :], lhsT=blk, rhs=blk, start=(t == 0), stop=(t == 3))
 
-        def gram_diag(b):
-            dg = stage.tile([P, 2, P], F32, tag="dg")
+        def gram_diag(g):
+            dg = stage.tile([P, 4, P], F32, tag="dg")
             nc.vector.tensor_tensor(
-                out=dg[:], in0=grams[b][:], in1=ident[:].unsqueeze(1).to_broadcast([P, 2, P]), op=ALU.mult
+                out=dg[:], in0=grams[g][:], in1=ident[:].unsqueeze(1).to_broadcast([P, 4, P]), op=ALU.mult
             )
-            nc.vector.tensor_reduce(out=n2[:, 2 * b:2 * b + 2], in_=dg[:], axis=AX.X, op=ALU.add)
+            nc.vector.tensor_reduce(out=n2[g][:], in_=dg[:], axis=AX.X, op=ALU.add)
+            nc.vector.tensor_scalar(out=n2c[g][:], in0=n2[g][:], scalar1=1e-14, scalar2=None, op0=ALU.max)
 
-        def c_root():
-            nc.vector.tensor_scalar(out=n2c[:], in0=n2[:], scalar1=1e-14, scalar2=None, op0=ALU.max)
-            nc.scalar.activation(out=y[:], in_=n2c[:], func=ACT.Sqrt, scale=0.01)
-            nc.scalar.activation(out=r1[:], in_=y[:], func=ACT.Relu, bias=ZMAX, scale=-1.0)
+        def c_pow(g):
+            nc.gpsimd.tensor_tensor(out=nrm[g][:], in0=n2c[g][:], in1=half[:, 0:4], op=ALU.pow)
 
-        def c_ln():
-            nc.scalar.activation(out=l1[:], in_=r1[:], func=ACT.Ln, bias=1.0 + ZMAX, scale=-1.0)
-            nc.scalar.activation(out=l2[:], in_=r1[:], func=ACT.Ln, bias=1.0 - ZMAX, scale=1.0)
+        def c_z(g):
+            nc.vector.tensor_scalar(
+                out=z[g][:], in0=nrm[g][:], scalar1=0.1, scalar2=1.0 - 1e-6, op0=ALU.mult, op1=ALU.min
+            )
+            nc.vector.reciprocal(out=rec[g][:], in_=nrm[g][:])
 
-        def c_rec():
-            nc.vector.reciprocal(out=rec[:], in_=y[:])
+        def c_ln(g):
+            nc.scalar.activation(out=l1[g][:], in_=z[g][:], func=ACT.Ln, bias=1.0, scale=1.0)
+            nc.scalar.activation(out=l2[g][:], in_=z[g][:], func=ACT.Ln, bias=1.0, scale=-1.0)
 
-        def c_s():
-            nc.vector.tensor_tensor(out=dl[:], in0=l1[:], in1=l2[:], op=ALU.subtract)
+        def c_s(g):
+            nc.vector.tensor_tensor(out=dl[g][:], in0=l1[g][:], in1=l2[g][:], op=ALU.subtract)
             nc.vector.scalar_tensor_tensor(
-                out=s[:], in0=dl[:], scalar=0.5, in1=rec[:], op0=ALU.mult, op1=ALU.mult
+                out=s[g][:], in0=dl[g][:], scalar=5.0, in1=rec[g][:], op0=ALU.mult, op1=ALU.mult
             )
 
         def spread(g):
-            sbc[g] = bank(g, [P, 4 * P])
+            sbc[g] = ps_hd.tile([P, 4 * P], F32, tag="hd", name="sbc")
             for mm in range(4):
                 nc.tensor.transpose(
-                    sbc[g][:, mm * P:(mm + 1) * P],
-                    s[:, 4 * g + mm:4 * g + mm + 1].to_broadcast([P, P]),
-                    ident[:],
+                    sbc[g][:, mm * P:(mm + 1) * P], s[g][:, mm:mm + 1].to_broadcast([P, P]), ident[:]
                 )
 
         def u_mul(h0, nh, bs):
@@ -168,7 +160,7 @@ def tile_pvconv2d_kernel(tc, x, Wk, bias, out):
                 )
 
         def bias_pe():
-            pb = bank(2, [P, O])
+            pb = ps_wt.tile([P, O], F32, tag="wt")
             nc.tensor.matmul(out=pb[:], lhsT=ones_bf[:], rhs=bias_row[:], start=True, stop=True)
             return pb
 
@@ -181,11 +173,10 @@ def tile_pvconv2d_kernel(tc, x, Wk, bias, out):
         wts = {}
         wgs = {}
 
-        def w_pe(n, hhs=(0, 1)):
-            k = KORD[n]
+        def w_pe(k, hhs=(0, 1)):
             wf = w_sb[k][:].bitcast(F32)
             for hh in hhs:
-                wt = bank(W_BANK[2 * n + hh], [P, 2, 2 * P])
+                wt = ps_wt.tile([P, 2, 2 * P], F32, tag="wt")
                 for u in range(2):
                     for o2 in range(2):
                         ot = 2 * hh + o2
@@ -196,8 +187,7 @@ def tile_pvconv2d_kernel(tc, x, Wk, bias, out):
                         )
                 wts[(k, hh)] = wt
 
-        def w_out(n, hh, eng):
-            k = KORD[n]
+        def w_out(k, hh, eng):
             if hh == 0:
                 wgs[k] = stage.tile([P, 4 * O], BF16, tag="wg", align_bytes=64, name="wg")
             dst = wgs[k][:].bitcast(F32)[:, hh * 512:(hh + 1) * 512].rearrange("p (c u) -> p c u", u=2)
@@ -207,8 +197,7 @@ def tile_pvconv2d_kernel(tc, x, Wk, bias, out):
             else:
                 nc.scalar.copy(out=dst, in_=src)
 
-        def w_quant(n):
-            k = KORD[n]
+        def w_quant(k):
             nc.vector.quantize_mx(out=wq[k][:].bitcast(FP8X4), scales=ws[k][:], in_=wgs[k][:])
 
         accs = {}
@@ -216,7 +205,10 @@ def tile_pvconv2d_kernel(tc, x, Wk, bias, out):
 
         def mx(T, ks):
             if T not in accs:
-                accs[T] = bank(ACC_BANK[T], [P, O])
+                if T in (3, 4):
+                    accs[T] = ps_hd.tile([P, O], F32, tag="hd", name="acc_hd")
+                else:
+                    accs[T] = ps_acc.tile([P, O], F32, tag="acc", name="acc")
                 done[T] = 0
             for k in ks:
                 done[T] += 1
@@ -234,53 +226,33 @@ def tile_pvconv2d_kernel(tc, x, Wk, bias, out):
 
         tl = {}
 
-        def tail_add(T):
-            t_sb = tpool.tile([P, O], F32, tag="t")
-            nc.vector.tensor_tensor(out=t_sb[:], in0=accs[T][:], in1=bias_bc[:], op=ALU.add)
-            tl[T] = t_sb
-
         def tail_a(T):
-            tail_add(T)
-            tail_ss(T)
-
-        def tail_ss(T):
-            t_sb = tl[T]
+            t_sb = stage.tile([P, O], F32, tag="t")
+            nc.vector.tensor_tensor(out=t_sb[:], in0=accs[T][:], in1=bias_bc[:], op=ALU.add)
             sq = stage.tile([P, O], F32, tag="sq")
             m2 = tsmall.tile([P, 1], F32, tag="m2")
             nc.vector.scalar_tensor_tensor(
                 out=sq[:], in0=t_sb[:], scalar=0.0, in1=t_sb[:], op0=ALU.max, op1=ALU.mult, accum_out=m2[:]
             )
-            tail_q(T, t_sb, m2, ACT.Relu)
-
-        def tail_ss_s(T):
-            t_sb = tl[T]
-            r_sb = tpool.tile([P, O], F32, tag="r")
-            nc.scalar.activation(out=r_sb[:], in_=t_sb[:], func=ACT.Relu)
-            sq = stage.tile([P, O], F32, tag="sq_s")
-            m2 = tsmall.tile([P, 1], F32, tag="m2")
-            nc.scalar.activation(out=sq[:], in_=r_sb[:], func=ACT.Square, accum_out=m2[:])
-            tail_q(T, r_sb, m2, ACT.Copy)
-
-        def tail_q(T, src, m2, func):
             a2 = tsmall.tile([P, 1], F32, tag="a2")
-            nc.gpsimd.tensor_scalar(out=a2[:], in0=m2[:], scalar1=1e-14, scalar2=0.01, op0=ALU.max, op1=ALU.mult)
+            nc.vector.tensor_scalar(out=a2[:], in0=m2[:], scalar1=1e-14, scalar2=0.01, op0=ALU.max, op1=ALU.mult)
             qv = tsmall.tile([P, 1], F32, tag="qv")
             nc.gpsimd.tensor_tensor(out=qv[:], in0=a2[:], in1=mhalf[:, 0:1], op=ALU.pow)
-            tl[T] = (src, a2, qv, func)
+            tl[T] = (t_sb, a2, qv)
 
         def tail_b(T):
-            t_sb, a2, qv, func = tl[T]
+            t_sb, a2, qv = tl[T]
             th = tsmall.tile([P, 1], F32, tag="th")
             nc.scalar.activation(out=th[:], in_=a2[:], func=ACT.Tanh, scale=qv[:, 0:1])
             gs = tsmall.tile([P, 1], F32, tag="gs")
             nc.scalar.activation(out=gs[:], in_=th[:], func=ACT.Copy, scale=qv[:, 0:1])
-            rs = rpool.tile([P, O], F32, tag="rs")
-            nc.scalar.activation(out=rs[:], in_=t_sb[:], func=func, scale=gs[:, 0:1])
+            rs = stage.tile([P, O], F32, tag="rs")
+            nc.scalar.activation(out=rs[:], in_=t_sb[:], func=ACT.Relu, scale=gs[:, 0:1])
             tl[T] = rs
 
         def tail_pe(T):
             rs = tl[T]
-            pt = bank(PT_BANK[T], [P, O])
+            pt = ps_wt.tile([P, O], F32, tag="wt")
             for ot in range(4):
                 nc.tensor.transpose(pt[:, ot * P:(ot + 1) * P], rs[:, ot * P:(ot + 1) * P], perm[:])
             tl[T] = pt
@@ -292,45 +264,6 @@ def tile_pvconv2d_kernel(tc, x, Wk, bias, out):
                 nc.vector.tensor_copy(out=dst, in_=src)
             else:
                 nc.scalar.copy(out=dst, in_=src)
-
-        lacc = {}
-        lm2 = {}
-
-        def last_mx(T, hf):
-            lacc[hf] = bank(LAST_BANK[hf], [P, O // 2])
-            for n, k in enumerate(KORD):
-                i, j = divmod(k, 3)
-                c0 = (2 * T + i) * ROW
-                nc.tensor.matmul_mx(
-                    out=lacc[hf][:],
-                    lhsT=uq[j][:, c0:c0 + P].bitcast(FP8X4),
-                    lhsT_scale=us[j][:, c0:c0 + P],
-                    rhs=wq[k][:, hf * 256:(hf + 1) * 256].bitcast(FP8X4),
-                    rhs_scale=ws[k][:, hf * 256:(hf + 1) * 256],
-                    start=(n == 0),
-                    stop=(n == NPOS - 1),
-                )
-
-        def last_a(T, hf):
-            if hf == 0:
-                tl[T] = tpool.tile([P, O], F32, tag="t", name="t_last")
-            cols = slice(hf * 256, (hf + 1) * 256)
-            nc.vector.tensor_tensor(out=tl[T][:, cols], in0=lacc[hf][:], in1=bias_bc[:, cols], op=ALU.add)
-            sq = stage.tile([P, O // 2], F32, tag="sq")
-            lm2[hf] = tsmall.tile([P, 1], F32, tag="lm2_%d" % hf, name="lm2")
-            nc.vector.scalar_tensor_tensor(
-                out=sq[:], in0=tl[T][:, cols], scalar=0.0, in1=tl[T][:, cols], op0=ALU.max, op1=ALU.mult,
-                accum_out=lm2[hf][:],
-            )
-
-        def last_m(T):
-            m2 = tsmall.tile([P, 1], F32, tag="m2")
-            nc.vector.tensor_tensor(out=m2[:], in0=lm2[0][:], in1=lm2[1][:], op=ALU.add)
-            a2 = tsmall.tile([P, 1], F32, tag="a2")
-            nc.vector.tensor_scalar(out=a2[:], in0=m2[:], scalar1=1e-14, scalar2=0.01, op0=ALU.max, op1=ALU.mult)
-            qv = tsmall.tile([P, 1], F32, tag="qv")
-            nc.gpsimd.tensor_tensor(out=qv[:], in0=a2[:], in1=mhalf[:, 0:1], op=ALU.pow)
-            tl[T] = (tl[T], a2, qv)
 
         def last_tile(T):
             t_sb, a2, qv = tl[T]
@@ -344,8 +277,8 @@ def tile_pvconv2d_kernel(tc, x, Wk, bias, out):
             nc.vector.tensor_scalar(
                 out=rs_b[:], in0=t_sb[:, 256:512], scalar1=gs[:, 0:1], scalar2=0.0, op0=ALU.mult, op1=ALU.max
             )
-            pt_a = bank(PT_BANK[T], [P, O // 2])
-            pt_b = bank(PT_BANK[T + 1], [P, O // 2])
+            pt_a = ps_wt.tile([P, O // 2], F32, tag="wt")
+            pt_b = ps_wt.tile([P, O // 2], F32, tag="wt")
             for o2 in range(2):
                 nc.tensor.transpose(pt_a[:, o2 * P:(o2 + 1) * P], rs_a[:, o2 * P:(o2 + 1) * P], perm[:])
             for o2 in range(2):
@@ -364,141 +297,133 @@ def tile_pvconv2d_kernel(tc, x, Wk, bias, out):
                 nc.sync.dma_start(out=out_v[b][:, :, q0:q1], in_=o_sb[:, b, :, q0:q1])
 
         gram_pe(0)
-        gram_diag(0)
         gram_pe(1)
-        gram_diag(1)
-        gram_pe(2)
-        gram_diag(2)
-        gram_pe(3)
         pb = bias_pe()
         bias_out(pb)
-        gram_diag(3)
-        c_root()
-        c_ln()
+        gram_diag(0)
+        c_pow(0)
+        gram_diag(1)
+        c_pow(1)
         w_pe(0)
-        w_out(0, 0, "v")
-        c_rec()
+        w_out(0, 0, "s")
         w_out(0, 1, "v")
         w_pe(1)
+        c_z(0)
+        c_ln(0)
         w_quant(0)
-        c_s()
+        c_s(0)
         w_pe(2, (0,))
         spread(0)
-        spread(1)
         w_out(1, 0, "s")
+        c_z(1)
+        c_ln(1)
         w_out(1, 1, "s")
         w_pe(2, (1,))
-        u_mul(0, 2, (0, 1, 2, 3))
-        u_quant(0, 2, (1,))
+        c_s(1)
+        spread(1)
         w_quant(1)
         w_out(2, 0, "s")
+        w_pe(3, (0,))
         w_out(2, 1, "s")
-        w_pe(3)
+        w_pe(3, (1,))
+        u_mul(0, 2, (0, 1, 2, 3))
+        u_quant(0, 2, (1,))
+        w_out(3, 0, "s")
         u_shift(0, 2)
-        mx(0, (1,))
+        w_quant(2)
+        w_out(3, 1, "s")
         u_quant(0, 2, (0, 2))
         w_pe(4)
+        mx(0, (1, 0, 2))
         u_mul(2, 2, (0, 1, 2, 3))
-        w_quant(2)
-        w_out(3, 0, "s")
-        w_out(3, 1, "s")
-        mx(0, (0,))
-        w_pe(5)
         u_quant(2, 2, (1,))
-        u_shift(2, 2)
-        u_quant(2, 2, (0, 2))
-        mx(0, (2,))
-        mx(1, (1, 0, 2))
-        w_quant(3)
         w_out(4, 0, "s")
+        u_shift(2, 2)
+        w_quant(3)
         w_out(4, 1, "s")
-        w_pe(6)
+        u_quant(2, 2, (0, 2))
+        mx(0, (3,))
+        w_pe(5)
+        mx(1, (1, 0, 2, 3))
         u_mul(4, 4, (0, 1, 2, 3))
+        w_quant(4)
         u_quant(4, 4, (1,))
         w_out(5, 0, "s")
         w_out(5, 1, "s")
+        u_shift(4, 4)
         mx(0, (4,))
         mx(1, (4,))
-        w_quant(4)
+        w_pe(6)
+        w_quant(5)
+        u_quant(4, 4, (0, 2))
         w_out(6, 0, "s")
         w_out(6, 1, "s")
-        w_pe(7)
-        u_shift(4, 4)
-        u_quant(4, 4, (0, 2))
-        mx(0, (3,))
-        mx(1, (3,))
-        mx(2, (1, 4, 0, 2, 3))
-        w_quant(5)
-        w_out(7, 0, "s")
-        w_pe(8)
-        w_out(7, 1, "s")
-        w_quant(6)
         mx(0, (5,))
         mx(1, (5,))
-        mx(2, (5,))
+        mx(2, (1, 4))
+        w_pe(7)
+        mx(2, (0, 2, 3, 5))
         u_mul(8, 4, (0, 1, 2, 3))
-        w_out(8, 0, "s")
-        w_out(8, 1, "s")
-        w_quant(7)
-        mx(0, (7,))
-        mx(1, (7,))
-        mx(2, (7,))
+        w_quant(6)
+        w_out(7, 0, "s")
+        w_out(7, 1, "s")
+        w_pe(8)
         u_quant(8, 4, (1,))
         u_shift(8, 4)
-        w_quant(8)
         mx(0, (6,))
         mx(1, (6,))
         mx(2, (6,))
+        w_quant(7)
+        w_out(8, 0, "s")
+        w_out(8, 1, "s")
+        u_mul(12, 4, (0, 1, 2, 3))
+        mx(0, (7,))
+        mx(1, (7,))
+        mx(2, (7,))
+        w_quant(8)
         u_quant(8, 4, (0, 2))
+        u_quant(12, 4, (1,))
+        u_shift(12, 4)
         mx(0, (8,))
         mx(1, (8,))
         mx(2, (8,))
-        tail_add(0)
-        mx(3, (1, 4, 0, 2, 3, 5, 7, 6, 8))
-        tail_ss_s(0)
-        tail_add(1)
-        tail_ss_s(1)
-        tail_add(2)
-        tail_ss_s(2)
-        u_mul(12, 4, (0, 1, 2, 3))
-        u_quant(12, 4, (1,))
-        u_shift(12, 4)
+        tail_a(0)
         tail_b(0)
-        u_quant(12, 4, (0, 2))
+        tail_a(1)
         tail_b(1)
-        tail_a(3)
+        u_quant(12, 4, (0, 2))
+        mx(3, range(9))
+        tail_a(2)
         tail_b(2)
-        tail_b(3)
         mx(4, range(9))
-        tail_a(4)
-        tail_b(4)
-        mx(5, range(9))
         tail_pe(0)
         tail_pe(1)
-        tail_a(5)
         tail_c(0)
         tail_c(1)
         store(0, 64)
-        tail_b(5)
+        tail_a(3)
+        tail_b(3)
+        mx(5, range(9))
+        tail_a(4)
+        tail_b(4)
         mx(6, range(9))
         tail_pe(2)
         tail_pe(3)
-        tail_pe(4)
-        tail_a(6)
         tail_c(2)
         tail_c(3)
         store(64, 128)
-        tail_c(4)
+        tail_a(5)
+        tail_b(5)
+        mx(7, range(9))
+        tail_a(6)
         tail_b(6)
-        last_mx(7, 0)
-        last_mx(7, 1)
-        last_a(7, 0)
+        tail_pe(4)
         tail_pe(5)
-        tail_pe(6)
-        last_a(7, 1)
-        last_m(7)
-        tail_c(5, "s")
+        tail_a(7)
+        tail_c(4, "s")
+        tail_c(5, "v")
         store(128, 192)
+        tail_pe(6)
         tail_c(6, "s")
         store(192, 224)
         last_tile(7)

from contextlib import ExitStack

import concourse.bass as bass
import concourse.mybir as mybir
import concourse.tile as tile
from concourse.masks import make_identity

F32 = mybir.dt.float32
BF16 = mybir.dt.bfloat16
U32 = mybir.dt.uint32
U8 = mybir.dt.uint8
I32 = mybir.dt.int32
FP8X4 = mybir.dt.float8_e4m3fn_x4
ALU = mybir.AluOpType
ACT = mybir.ActivationFunctionType
AX = mybir.AxisListType

P = 128
B, C, O, H, W = 4, 512, 512, 16, 16
HW = H * W
ROW = B * W
NPOS = 9
FLOPS = 2 * B * HW * C * NPOS * O


def tile_pvconv2d_kernel(tc, x, Wk, bias, out):
    nc = tc.nc
    with ExitStack() as ctx:
        const = ctx.enter_context(tc.tile_pool(name="const", bufs=1))
        big = ctx.enter_context(tc.tile_pool(name="big", bufs=1))
        stage = ctx.enter_context(tc.tile_pool(name="stage", bufs=3))
        small = ctx.enter_context(tc.tile_pool(name="small", bufs=1))
        tsmall = ctx.enter_context(tc.tile_pool(name="tsmall", bufs=4))
        ps_hd = ctx.enter_context(tc.psum_pool(name="ps_hd", bufs=2))
        ps_wt = ctx.enter_context(tc.psum_pool(name="ps_wt", bufs=3))
        ps_acc = ctx.enter_context(tc.psum_pool(name="ps_acc", bufs=3))

        x_sb = big.tile([P, B, 4, HW], BF16)
        w_sb = [big.tile([P, 4 * C], BF16, name="w_sb%d" % k) for k in range(NPOS)]
        wq = [big.tile([P, O], U32, name="wq%d" % k, align_bytes=64) for k in range(NPOS)]
        ws = [big.tile([P, O], U8, name="ws%d" % k, align_bytes=64) for k in range(NPOS)]
        g_t = [big.tile([P, H, B, W, 4], BF16, name="g%d" % j, align_bytes=64) for j in range(3)]
        uq = [big.tile([P, (H + 2) * ROW], U32, name="uq%d" % j, align_bytes=64) for j in range(3)]
        us = [big.tile([P, (H + 2) * ROW], U8, name="us%d" % j, align_bytes=64) for j in range(3)]
        o_sb = big.tile([P, B, 4, HW], F32)
        out_v = out.rearrange("b (n ot) h w -> b n ot (h w)", ot=4)
        ident = const.tile([P, P], F32)
        perm = const.tile([P, P], F32)
        half = const.tile([P, 8], F32)
        mhalf = const.tile([P, 8], F32)
        ones_bf = const.tile([P, P], BF16)
        bias_row = const.tile([P, O], BF16)
        bias_bc = const.tile([P, O], F32)
        junk = const.tile([P, 8], F32)
        flat = [g_t[j][:].rearrange("p h b w t -> p (h b) (w t)") for j in range(3)]
        line = [g_t[j][:].rearrange("p h b w t -> p (h b w t)") for j in range(3)]

        for b in range(B):
            nc.sync.dma_start(
                out=x_sb[:, b].rearrange("p (u e) q -> p u (e q)", u=2),
                in_=x[b].rearrange("(u p e) h w -> p u (e h w)", u=2, e=2),
            )
        for k in range(NPOS):
            nc.sync.dma_start(out=w_sb[k][:], in_=Wk[k].rearrange("(n ot) c -> n (ot c)", ot=4))
        make_identity(nc, ident[:])
        nc.gpsimd.memset(half[:], 0.5)
        nc.gpsimd.memset(mhalf[:], -0.5)
        nc.gpsimd.memset(bias_row[:], 0.0)
        nc.scalar.dma_start(out=bias_row[0:1, :], in_=bias.unsqueeze(0))
        nc.gpsimd.memset(ones_bf[:], 1.0)
        nc.gpsimd.tensor_copy(
            out=perm[:].rearrange("p (b hh w) -> p b hh w", b=B, hh=2),
            in_=ident[:].rearrange("p (hh b w) -> p b hh w", hh=2, b=B),
        )
        nc.scalar.activation(out=junk[:], in_=half[:], func=ACT.Ln)
        for j in range(3):
            nc.vector.memset(us[j][:].bitcast(I32), 0)
            nc.vector.memset(uq[j][:, 0:ROW].bitcast(I32), 0)
            nc.vector.memset(uq[j][:, (H + 1) * ROW:(H + 2) * ROW].bitcast(I32), 0)
        nc.vector.memset(g_t[0][:], 0.0)
        nc.vector.memset(g_t[2][:], 0.0)

        n2 = [small.tile([P, 4], F32, name="n2_%d" % g) for g in range(2)]
        n2c = [small.tile([P, 4], F32, name="n2c_%d" % g) for g in range(2)]
        nrm = [small.tile([P, 4], F32, name="nrm_%d" % g) for g in range(2)]
        z = [small.tile([P, 4], F32, name="z_%d" % g) for g in range(2)]
        l1 = [small.tile([P, 4], F32, name="l1_%d" % g) for g in range(2)]
        l2 = [small.tile([P, 4], F32, name="l2_%d" % g) for g in range(2)]
        rec = [small.tile([P, 4], F32, name="rec_%d" % g) for g in range(2)]
        dl = [small.tile([P, 4], F32, name="dl_%d" % g) for g in range(2)]
        s = [small.tile([P, 4], F32, name="s_%d" % g) for g in range(2)]
        grams = {}
        sbc = {}

        def gram_pe(g):
            grams[g] = ps_hd.tile([P, 4, P], F32, tag="hd", name="gram")
            for mm in range(4):
                b, hf = divmod(4 * g + mm, 2)
                for t in range(4):
                    blk = x_sb[:, b, t, hf * P:(hf + 1) * P]
                    nc.tensor.matmul(out=grams[g][:, mm, :], lhsT=blk, rhs=blk, start=(t == 0), stop=(t == 3))

        def gram_diag(g):
            dg = stage.tile([P, 4, P], F32, tag="dg")
            nc.vector.tensor_tensor(
                out=dg[:], in0=grams[g][:], in1=ident[:].unsqueeze(1).to_broadcast([P, 4, P]), op=ALU.mult
            )
            nc.vector.tensor_reduce(out=n2[g][:], in_=dg[:], axis=AX.X, op=ALU.add)
            nc.vector.tensor_scalar(out=n2c[g][:], in0=n2[g][:], scalar1=1e-14, scalar2=None, op0=ALU.max)

        def c_pow(g):
            nc.gpsimd.tensor_tensor(out=nrm[g][:], in0=n2c[g][:], in1=half[:, 0:4], op=ALU.pow)

        def c_z(g):
            nc.vector.tensor_scalar(
                out=z[g][:], in0=nrm[g][:], scalar1=0.1, scalar2=1.0 - 1e-6, op0=ALU.mult, op1=ALU.min
            )
            nc.vector.reciprocal(out=rec[g][:], in_=nrm[g][:])

        def c_ln(g):
            nc.scalar.activation(out=l1[g][:], in_=z[g][:], func=ACT.Ln, bias=1.0, scale=1.0)
            nc.scalar.activation(out=l2[g][:], in_=z[g][:], func=ACT.Ln, bias=1.0, scale=-1.0)

        def c_s(g):
            nc.vector.tensor_tensor(out=dl[g][:], in0=l1[g][:], in1=l2[g][:], op=ALU.subtract)
            nc.vector.scalar_tensor_tensor(
                out=s[g][:], in0=dl[g][:], scalar=5.0, in1=rec[g][:], op0=ALU.mult, op1=ALU.mult
            )

        def spread(g):
            sbc[g] = ps_hd.tile([P, 4 * P], F32, tag="hd", name="sbc")
            for mm in range(4):
                nc.tensor.transpose(
                    sbc[g][:, mm * P:(mm + 1) * P], s[g][:, mm:mm + 1].to_broadcast([P, P]), ident[:]
                )

        def u_mul(h0, nh, bs):
            for b in bs:
                nc.vector.tensor_tensor(
                    out=g_t[1][:, h0:h0 + nh, b, :, :],
                    in0=x_sb[:, b, :, h0 * W:(h0 + nh) * W].rearrange("p t (h w) -> p h w t", h=nh),
                    in1=sbc[b // 2][:, (b % 2) * HW + h0 * W:(b % 2) * HW + (h0 + nh) * W]
                    .rearrange("p (h w) -> p h w", h=nh)
                    .unsqueeze(3)
                    .to_broadcast([P, nh, W, 4]),
                    op=ALU.mult,
                )

        def u_shift(h0, nh):
            r0, r1 = h0 * B, (h0 + nh) * B
            nc.scalar.copy(out=flat[0][:, r0:r1, 4:64], in_=flat[1][:, r0:r1, 0:60])
            nc.scalar.copy(out=flat[2][:, r0:r1, 0:60], in_=flat[1][:, r0:r1, 4:64])

        def u_quant(h0, nh, js):
            for j in js:
                nc.vector.quantize_mx(
                    out=uq[j][:, (h0 + 1) * ROW:(h0 + nh + 1) * ROW].bitcast(FP8X4),
                    scales=us[j][:, (h0 + 1) * ROW:(h0 + nh + 1) * ROW],
                    in_=line[j][:, h0 * ROW * 4:(h0 + nh) * ROW * 4],
                )

        def bias_pe():
            pb = ps_wt.tile([P, O], F32, tag="wt")
            nc.tensor.matmul(out=pb[:], lhsT=ones_bf[:], rhs=bias_row[:], start=True, stop=True)
            return pb

        def bias_out(pb):
            nc.scalar.copy(
                out=bias_bc[:].rearrange("p (ot n) -> p ot n", ot=4),
                in_=pb[:].rearrange("p (n ot) -> p ot n", ot=4),
            )

        wts = {}
        wgs = {}

        def w_pe(k, hhs=(0, 1)):
            wf = w_sb[k][:].bitcast(F32)
            for hh in hhs:
                wt = ps_wt.tile([P, 2, 2 * P], F32, tag="wt")
                for u in range(2):
                    for o2 in range(2):
                        ot = 2 * hh + o2
                        nc.tensor.transpose(
                            wt[:, u, o2 * P:(o2 + 1) * P],
                            wf[:, 256 * ot + P * u:256 * ot + P * u + P],
                            ident[:],
                        )
                wts[(k, hh)] = wt

        def w_out(k, hh, eng):
            if hh == 0:
                wgs[k] = stage.tile([P, 4 * O], BF16, tag="wg", align_bytes=64, name="wg")
            dst = wgs[k][:].bitcast(F32)[:, hh * 512:(hh + 1) * 512].rearrange("p (c u) -> p c u", u=2)
            src = wts[(k, hh)][:].rearrange("p u c -> p c u")
            if eng == "v":
                nc.vector.tensor_copy(out=dst, in_=src)
            else:
                nc.scalar.copy(out=dst, in_=src)

        def w_quant(k):
            nc.vector.quantize_mx(out=wq[k][:].bitcast(FP8X4), scales=ws[k][:], in_=wgs[k][:])

        accs = {}
        done = {}

        def mx(T, ks):
            if T not in accs:
                if T in (3, 4):
                    accs[T] = ps_hd.tile([P, O], F32, tag="hd", name="acc_hd")
                else:
                    accs[T] = ps_acc.tile([P, O], F32, tag="acc", name="acc")
                done[T] = 0
            for k in ks:
                done[T] += 1
                i, j = divmod(k, 3)
                c0 = (2 * T + i) * ROW
                nc.tensor.matmul_mx(
                    out=accs[T][:],
                    lhsT=uq[j][:, c0:c0 + P].bitcast(FP8X4),
                    lhsT_scale=us[j][:, c0:c0 + P],
                    rhs=wq[k][:].bitcast(FP8X4),
                    rhs_scale=ws[k][:],
                    start=(done[T] == 1),
                    stop=(done[T] == NPOS),
                )

        tl = {}

        def tail_a(T):
            t_sb = stage.tile([P, O], F32, tag="t")
            nc.vector.tensor_tensor(out=t_sb[:], in0=accs[T][:], in1=bias_bc[:], op=ALU.add)
            sq = stage.tile([P, O], F32, tag="sq")
            m2 = tsmall.tile([P, 1], F32, tag="m2")
            nc.vector.scalar_tensor_tensor(
                out=sq[:], in0=t_sb[:], scalar=0.0, in1=t_sb[:], op0=ALU.max, op1=ALU.mult, accum_out=m2[:]
            )
            a2 = tsmall.tile([P, 1], F32, tag="a2")
            nc.vector.tensor_scalar(out=a2[:], in0=m2[:], scalar1=1e-14, scalar2=0.01, op0=ALU.max, op1=ALU.mult)
            qv = tsmall.tile([P, 1], F32, tag="qv")
            nc.gpsimd.tensor_tensor(out=qv[:], in0=a2[:], in1=mhalf[:, 0:1], op=ALU.pow)
            tl[T] = (t_sb, a2, qv)

        def tail_b(T):
            t_sb, a2, qv = tl[T]
            th = tsmall.tile([P, 1], F32, tag="th")
            nc.scalar.activation(out=th[:], in_=a2[:], func=ACT.Tanh, scale=qv[:, 0:1])
            gs = tsmall.tile([P, 1], F32, tag="gs")
            nc.scalar.activation(out=gs[:], in_=th[:], func=ACT.Copy, scale=qv[:, 0:1])
            rs = stage.tile([P, O], F32, tag="rs")
            nc.scalar.activation(out=rs[:], in_=t_sb[:], func=ACT.Relu, scale=gs[:, 0:1])
            tl[T] = rs

        def tail_pe(T):
            rs = tl[T]
            pt = ps_wt.tile([P, O], F32, tag="wt")
            for ot in range(4):
                nc.tensor.transpose(pt[:, ot * P:(ot + 1) * P], rs[:, ot * P:(ot + 1) * P], perm[:])
            tl[T] = pt

        def tail_c(T, eng="s"):
            dst = o_sb[:, :, :, 32 * T:32 * T + 32]
            src = tl[T][:].rearrange("p (ot b q) -> p b ot q", ot=4, b=B)
            if eng == "v":
                nc.vector.tensor_copy(out=dst, in_=src)
            else:
                nc.scalar.copy(out=dst, in_=src)

        def last_tile(T):
            t_sb, a2, qv = tl[T]
            th = tsmall.tile([P, 1], F32, tag="th")
            nc.scalar.activation(out=th[:], in_=a2[:], func=ACT.Tanh, scale=qv[:, 0:1])
            gs = tsmall.tile([P, 1], F32, tag="gs")
            nc.scalar.activation(out=gs[:], in_=th[:], func=ACT.Copy, scale=qv[:, 0:1])
            rs_a = stage.tile([P, O // 2], F32, tag="rs_a")
            rs_b = stage.tile([P, O // 2], F32, tag="rs_b")
            nc.scalar.activation(out=rs_a[:], in_=t_sb[:, 0:256], func=ACT.Relu, scale=gs[:, 0:1])
            nc.vector.tensor_scalar(
                out=rs_b[:], in0=t_sb[:, 256:512], scalar1=gs[:, 0:1], scalar2=0.0, op0=ALU.mult, op1=ALU.max
            )
            pt_a = ps_wt.tile([P, O // 2], F32, tag="wt")
            pt_b = ps_wt.tile([P, O // 2], F32, tag="wt")
            for o2 in range(2):
                nc.tensor.transpose(pt_a[:, o2 * P:(o2 + 1) * P], rs_a[:, o2 * P:(o2 + 1) * P], perm[:])
            for o2 in range(2):
                nc.tensor.transpose(pt_b[:, o2 * P:(o2 + 1) * P], rs_b[:, o2 * P:(o2 + 1) * P], perm[:])
            nc.scalar.copy(
                out=o_sb[:, :, 0:2, 32 * T:32 * T + 32],
                in_=pt_a[:].rearrange("p (ot b q) -> p b ot q", ot=2, b=B),
            )
            nc.vector.tensor_copy(
                out=o_sb[:, :, 2:4, 32 * T:32 * T + 32],
                in_=pt_b[:].rearrange("p (ot b q) -> p b ot q", ot=2, b=B),
            )

        def store(q0, q1):
            for b in range(B):
                nc.sync.dma_start(out=out_v[b][:, :, q0:q1], in_=o_sb[:, b, :, q0:q1])

        gram_pe(0)
        gram_pe(1)
        pb = bias_pe()
        bias_out(pb)
        gram_diag(0)
        c_pow(0)
        gram_diag(1)
        c_pow(1)
        w_pe(0)
        w_out(0, 0, "s")
        w_out(0, 1, "v")
        w_pe(1)
        c_z(0)
        c_ln(0)
        w_quant(0)
        c_s(0)
        w_pe(2, (0,))
        spread(0)
        w_out(1, 0, "s")
        c_z(1)
        c_ln(1)
        w_out(1, 1, "s")
        w_pe(2, (1,))
        c_s(1)
        spread(1)
        w_quant(1)
        w_out(2, 0, "s")
        w_pe(3, (0,))
        w_out(2, 1, "s")
        w_pe(3, (1,))
        u_mul(0, 2, (0, 1, 2, 3))
        u_quant(0, 2, (1,))
        w_out(3, 0, "s")
        u_shift(0, 2)
        w_quant(2)
        w_out(3, 1, "s")
        u_quant(0, 2, (0, 2))
        w_pe(4)
        mx(0, (1, 0, 2))
        u_mul(2, 2, (0, 1, 2, 3))
        u_quant(2, 2, (1,))
        w_out(4, 0, "s")
        u_shift(2, 2)
        w_quant(3)
        w_out(4, 1, "s")
        u_quant(2, 2, (0, 2))
        mx(0, (3,))
        w_pe(5)
        mx(1, (1, 0, 2, 3))
        u_mul(4, 4, (0, 1, 2, 3))
        w_quant(4)
        u_quant(4, 4, (1,))
        w_out(5, 0, "s")
        w_out(5, 1, "s")
        u_shift(4, 4)
        mx(0, (4,))
        mx(1, (4,))
        w_pe(6)
        w_quant(5)
        u_quant(4, 4, (0, 2))
        w_out(6, 0, "s")
        w_out(6, 1, "s")
        mx(0, (5,))
        mx(1, (5,))
        mx(2, (1, 4))
        w_pe(7)
        mx(2, (0, 2, 3, 5))
        u_mul(8, 4, (0, 1, 2, 3))
        w_quant(6)
        w_out(7, 0, "s")
        w_out(7, 1, "s")
        w_pe(8)
        u_quant(8, 4, (1,))
        u_shift(8, 4)
        mx(0, (6,))
        mx(1, (6,))
        mx(2, (6,))
        w_quant(7)
        w_out(8, 0, "s")
        w_out(8, 1, "s")
        u_mul(12, 4, (0, 1, 2, 3))
        mx(0, (7,))
        mx(1, (7,))
        mx(2, (7,))
        w_quant(8)
        u_quant(8, 4, (0, 2))
        u_quant(12, 4, (1,))
        u_shift(12, 4)
        mx(0, (8,))
        mx(1, (8,))
        mx(2, (8,))
        tail_a(0)
        tail_b(0)
        tail_a(1)
        tail_b(1)
        u_quant(12, 4, (0, 2))
        mx(3, range(9))
        tail_a(2)
        tail_b(2)
        mx(4, range(9))
        tail_pe(0)
        tail_pe(1)
        tail_c(0)
        tail_c(1)
        store(0, 64)
        tail_a(3)
        tail_b(3)
        mx(5, range(9))
        tail_a(4)
        tail_b(4)
        mx(6, range(9))
        tail_pe(2)
        tail_pe(3)
        tail_c(2)
        tail_c(3)
        store(64, 128)
        tail_a(5)
        tail_b(5)
        mx(7, range(9))
        tail_a(6)
        tail_b(6)
        tail_pe(4)
        tail_pe(5)
        tail_a(7)
        tail_c(4, "s")
        tail_c(5, "v")
        store(128, 192)
        tail_pe(6)
        tail_c(6, "s")
        store(192, 224)
        last_tile(7)
        store(224, 256)
